import numpy as np
import ml_dtypes


def mxq(x, axis, fmt="e4m3"):
    dtype, down = {"e4m3": (ml_dtypes.float8_e4m3fn, 7), "e5m2": (ml_dtypes.float8_e5m2, 14)}[fmt]
    v = np.moveaxis(np.asarray(x, np.float32).astype(ml_dtypes.bfloat16).astype(np.float64), axis, -1)
    blocks = v.reshape(v.shape[:-1] + (-1, 32))
    amax = np.abs(blocks).max(-1, keepdims=True)
    byte = np.maximum(np.where(amax > 0, np.frexp(amax)[1] - 1 + 127, 0) - down, 1)
    scale = np.exp2(byte - 127.0)
    codes = (blocks / scale).astype(np.float32).astype(dtype).astype(np.float64)
    return np.moveaxis((codes * scale).reshape(v.shape), -1, axis)


WIDE = False


def mx_kscale(k):
    if not WIDE:
        return np.ones(k)
    levels = np.array([10, -10, 5, -5, 0])
    a = np.random.permutation(np.resize(levels, k // 512 * 4)).reshape(k // 512, 4)
    idx = np.arange(k)
    return np.exp2(a[idx // 512, idx % 128 // 32])


BF16 = ml_dtypes.bfloat16


def bf(x):
    return np.asarray(x, np.float32).astype(BF16)


def f64(x):
    return np.asarray(x).astype(np.float64)


E2M1 = np.array([0.0, 0.5, 1.0, 1.5, 2.0, 3.0, 4.0, 6.0, -0.0, -0.5, -1.0, -1.5, -2.0, -3.0, -4.0, -6.0])


def pack_weight(w, fmt):
    k, n = w.shape
    w = f64(bf(w)).reshape(k // 32, 32, n)
    amax = np.abs(w).max(1)
    if fmt == "e4m3":
        byte = np.frexp(amax)[1] - 1 + 127 - 7
    else:
        mant, ex = np.frexp(amax / 6.0)
        byte = np.where(mant > 0.5, ex, ex - 1) + 127
    byte = np.clip(np.where(amax > 0, byte, 1), 1, 254)
    scaled = (w * np.exp2(127.0 - byte)[:, None, :]).reshape(k, n).astype(np.float32)
    by_word = np.ascontiguousarray(scaled.reshape(k // 512, 128, 4, n).transpose(0, 1, 3, 2))
    if fmt == "e4m3":
        words = by_word.astype(ml_dtypes.float8_e4m3fn).view(np.uint8)
    else:
        c = by_word.astype(ml_dtypes.float4_e2m1fn).view(np.uint8) & 0xF
        words = c[..., 0::2] | (c[..., 1::2] << 4)
    return np.ascontiguousarray(words), np.ascontiguousarray(byte.astype(np.uint8).reshape(k // 512, 16, n))


def unpack_weight(words, scales, fmt):
    g, p, n, _ = words.shape
    if fmt == "e4m3":
        vals = np.ascontiguousarray(words).view(ml_dtypes.float8_e4m3fn).astype(np.float64)
    else:
        nib = np.empty((g, p, n, 4), np.uint8)
        nib[..., 0::2] = words & 0xF
        nib[..., 1::2] = words >> 4
        vals = E2M1[nib]
    vals = vals * np.repeat(np.exp2(scales.astype(np.float64) - 127.0), 8, axis=1)[..., None]
    return vals.transpose(0, 1, 3, 2).reshape(g * 512, n)


B, N, E, L, A, H1, H2, G = 256, 8, 8, 384, 128, 1024, 1024, 8
D = L + A
EPS = 1e-5


def mish(v):
    return v * np.tanh(np.log(1.0 + np.exp(v)))


def layer_norm(v, gamma, beta):
    mu = v.mean(-1, keepdims=True)
    var = v.var(-1, keepdims=True)
    return (v - mu) / np.sqrt(var + EPS) * gamma + beta


def setup_inputs():
    s = mx_kscale(D)
    r = np.random.standard_normal
    tokens = bf(r((B, N, D)) * s)
    logits = bf(r((B, N, E)))
    stack = r((E, D, H1)) / np.sqrt(D) / s[:, None]
    W1_words, W1_scales = pack_weight(stack.reshape(-1, H1), "e4m3")
    return {"tokens": tokens,
            "logits": logits,
            "W1_words": W1_words,
            "W1_scales": W1_scales,
            "b1": bf(0.1 * r((E, H1))),
            "g1": bf(1.0 + 0.1 * r((E, H1))),
            "be1": bf(0.1 * r((E, H1)))}


def reference(tokens, logits, W1_words, W1_scales, b1, g1, be1):
    tok, lg = f64(tokens), f64(logits)
    ex = np.exp(lg - lg.max(1, keepdims=True))
    disp = ex / ex.sum(1, keepdims=True)
    slot = sum(disp[:, n, :].T[:, :, None] * tok[None, :, n, :] for n in range(N))
    h = (mxq(slot, 2, "e4m3") @ unpack_weight(W1_words, W1_scales, "e4m3").reshape(E, D, H1)) + f64(b1)[:, None, :]
    h = mish(layer_norm(h, f64(g1)[:, None, :], f64(be1)[:, None, :]))
    return h.transpose(1, 0, 2)

@@ -1,0 +1,344 @@
+from contextlib import ExitStack
+
+import concourse.mybir as mybir
+from concourse.masks import make_identity
+
+F32 = mybir.dt.float32
+BF16 = mybir.dt.bfloat16
+I32 = mybir.dt.int32
+U32 = mybir.dt.uint32
+U8 = mybir.dt.uint8
+FP8X4 = mybir.dt.float8_e4m3fn_x4
+ALU = mybir.AluOpType
+ACT = mybir.ActivationFunctionType
+AX = mybir.AxisListType
+
+P = 128
+BATCH_ROWS = 256
+AGENTS = 8
+EXPERTS = 8
+D = 512
+H = 1024
+EPS = 1e-5
+PACK = 4
+BANK = 512
+B_TILES = BATCH_ROWS // P
+CHUNKS = H // P
+
+PE_EXPERTS = 6
+POOL_EXPERTS = EXPERTS - PE_EXPERTS
+SPLIT = 2
+GROUP_B = P // (AGENTS * SPLIT)
+GROUPS = P // GROUP_B
+BANK_GROUPS = 2
+ROUTE_BANKS = GROUPS // BANK_GROUPS
+UNITS_PER_ROUND = 4
+
+FLOPS = 2 * BATCH_ROWS * EXPERTS * D * H + 2 * BATCH_ROWS * AGENTS * EXPERTS * D
+
+
+def tile_softmoedynamics_pa_e_kernel(tc, tokens, logits, W1_words, W1_scales, b1, g1, be1, out):
+    nc = tc.nc
+    with ExitStack() as ctx:
+        ctx.enter_context(tc.manual_schedule())
+        keep = ctx.enter_context(tc.tile_pool(name="keep", bufs=1))
+        token_pool = ctx.enter_context(tc.tile_pool(name="token_pool", bufs=1))
+        pool_work = ctx.enter_context(tc.tile_pool(name="pool_work", bufs=2))
+        work = ctx.enter_context(tc.tile_pool(name="work", bufs=8))
+        small = ctx.enter_context(tc.tile_pool(name="small", bufs=8))
+        psum = ctx.enter_context(tc.psum_pool(name="psum", bufs=8))
+
+        logits_bf = keep.tile([P, B_TILES, AGENTS, EXPERTS], BF16)
+        nc.sync.dma_start(out=logits_bf[:], in_=logits.rearrange("(t p) n e -> p t n e", p=P))
+
+        rows_gain = keep.tile([P, P], BF16)
+        rows_bias = keep.tile([P, P], BF16)
+        half_rows = EXPERTS * CHUNKS
+        nc.vector.memset(rows_bias[half_rows:P, :], 0.0)
+        nc.sync.dma_start(out=rows_bias[0:half_rows, :], in_=b1.rearrange("e (c p) -> (e c) p", p=P))
+        nc.sync.dma_start(out=rows_gain[0:half_rows, :], in_=g1.rearrange("e (c p) -> (e c) p", p=P))
+        nc.sync.dma_start(out=rows_gain[half_rows:P, :], in_=be1.rearrange("e (c p) -> (e c) p", p=P))
+
+        def load_token_pairs(bt):
+            pairs = token_pool.tile([P, GROUPS, D], BF16, tag="pairs", name="pairs%d" % bt)
+            rows = tokens[bt * P : (bt + 1) * P].rearrange("(g b) n d -> (b n) g d", b=GROUP_B)
+            for s in range(SPLIT):
+                nc.sync.dma_start(out=pairs[s:P:SPLIT, :, :], in_=rows)
+            return pairs
+
+        def load_token_rows(bt):
+            by_row = token_pool.tile([P, AGENTS, D], BF16, tag="by_row", name="by_row%d" % bt)
+            nc.sync.dma_start(out=by_row[:], in_=tokens[bt * P : (bt + 1) * P])
+            return by_row
+
+        token_pairs = {0: load_token_pairs(0)}
+        token_rows = {0: load_token_rows(0)}
+
+        w_planes = keep.tile([P, EXPERTS, H], U8, align_bytes=64)
+        nc.vector.memset(w_planes[:].rearrange("p e n -> p (e n)").bitcast(I32), 0)
+        for quad in range(4):
+            nc.sync.dma_start(
+                out=w_planes[32 * quad : 32 * quad + 4, :, :].bitcast(I32),
+                in_=W1_scales[:, 4 * quad : 4 * quad + 4, :].rearrange("g r n -> r g n").bitcast(I32),
+            )
+        w_words = keep.tile([P, EXPERTS, H], U32, align_bytes=64)
+        for e in range(EXPERTS):
+            nc.sync.dma_start(
+                out=w_words[:, e, :].bitcast(I32),
+                in_=W1_words[e].rearrange("p n t -> p (n t)").bitcast(I32),
+            )
+
+        ident = keep.tile([P, P], BF16)
+        make_identity(nc, ident[:])
+        eps_col = keep.tile([P, 1], F32)
+        nc.vector.memset(eps_col[:], EPS)
+        one_col = keep.tile([P, 1], F32)
+        nc.vector.memset(one_col[:], 1.0)
+        warm = keep.tile([P, 1], F32)
+        nc.scalar.activation(out=warm[:], in_=one_col[:], func=ACT.Exp)
+        same_row = keep.tile([P, GROUP_B], F32)
+        nc.vector.tensor_reduce(
+            out=same_row[:], in_=ident[:].rearrange("p (g b) -> p b g", b=GROUP_B), axis=AX.X, op=ALU.add
+        )
+
+        by_expert = logits_bf[:].rearrange("p t n e -> p t e n")
+        wide = [P, B_TILES, EXPERTS, AGENTS]
+        top = keep.tile([P, B_TILES, EXPERTS], F32)
+        nc.vector.tensor_reduce(out=top[:], in_=by_expert, axis=AX.X, op=ALU.max)
+        shifted = keep.tile(wide, F32)
+        nc.vector.tensor_tensor(
+            out=shifted[:], in0=by_expert, in1=top[:].unsqueeze(3).to_broadcast(wide), op=ALU.subtract
+        )
+        grown = keep.tile(wide, F32)
+        nc.scalar.activation(out=grown[:], in_=shifted[:], func=ACT.Exp)
+        total = keep.tile([P, B_TILES, EXPERTS], F32)
+        nc.vector.tensor_reduce(out=total[:], in_=grown[:], axis=AX.X, op=ALU.add)
+        inverse = keep.tile([P, B_TILES, EXPERTS], F32)
+        nc.vector.reciprocal(out=inverse[:], in_=total[:])
+        disp = keep.tile(wide, F32)
+        nc.vector.tensor_tensor(
+            out=disp[:], in0=grown[:], in1=inverse[:].unsqueeze(3).to_broadcast(wide), op=ALU.mult
+        )
+        hi_lo = keep.tile(wide + [SPLIT], BF16)
+        nc.vector.tensor_copy(out=hi_lo[:, :, :, :, 0], in_=disp[:])
+        nc.vector.tensor_tensor(out=hi_lo[:, :, :, :, 1], in0=disp[:], in1=hi_lo[:, :, :, :, 0], op=ALU.subtract)
+
+        def rows_to_columns(rows, name):
+            turned = psum.tile([P, P], BF16, tag="bank", name="turned_" + name)
+            nc.tensor.transpose(out=turned[:], in_=rows[:], identity=ident[:])
+            columns = keep.tile([P, P], BF16, name="columns_" + name)
+            nc.scalar.copy(out=columns[:], in_=turned[:])
+            return columns
+
+        def spread_vector(columns, first, name):
+            bank = psum.tile([P, H], BF16, tag="bank", name=name)
+            for c in range(CHUNKS):
+                nc.tensor.transpose(
+                    out=bank[:, c * P : (c + 1) * P],
+                    in_=columns[:, first + c : first + c + 1].to_broadcast([P, P]),
+                    identity=ident[:],
+                )
+            return bank
+
+        columns_bias = rows_to_columns(rows_bias, "bias")
+        columns_gain = rows_to_columns(rows_gain, "gain")
+        bias_all = keep.tile([P, EXPERTS, H], BF16)
+        for e in range(EXPERTS):
+            bias_bank = spread_vector(columns_bias, e * CHUNKS, "bias_bank")
+            nc.scalar.copy(out=bias_all[:, e, :], in_=bias_bank[:])
+
+        grouped = {}
+        codes = {}
+        slot_planes = {}
+        for bt in range(B_TILES):
+            grouped[bt] = keep.tile([P, EXPERTS, P, PACK], BF16, align_bytes=64, name="grouped%d" % bt)
+            codes[bt] = keep.tile([P, EXPERTS, P], U32, align_bytes=64, name="codes%d" % bt)
+            slot_planes[bt] = keep.tile([P, EXPERTS, P], U8, align_bytes=64, name="slot_planes%d" % bt)
+
+        def block_diagonal_weights(bt):
+            shape = [P, PE_EXPERTS, GROUP_B, AGENTS * SPLIT]
+            masked = keep.tile(shape, BF16, name="masked%d" % bt)
+            nc.vector.tensor_tensor(
+                out=masked[:],
+                in0=hi_lo[:, bt, 0:PE_EXPERTS].rearrange("p e n s -> p e (n s)").unsqueeze(2).to_broadcast(shape),
+                in1=same_row[:].unsqueeze(1).unsqueeze(3).to_broadcast(shape),
+                op=ALU.mult,
+            )
+            turned = psum.tile([P, PE_EXPERTS, P], BF16, tag="bank", name="turned_weights")
+            for e in range(PE_EXPERTS):
+                nc.tensor.transpose(
+                    out=turned[:, e, :], in_=masked[:, e].rearrange("p b c -> p (b c)"), identity=ident[:]
+                )
+            diagonal = keep.tile([P, PE_EXPERTS, P], BF16, name="diagonal%d" % bt)
+            nc.scalar.copy(out=diagonal[:], in_=turned[:])
+            return diagonal
+
+        def tensor_slots(bt, bank_index, diagonal):
+            rows = BANK_GROUPS * GROUP_B
+            sums = psum.tile([P, PACK, PE_EXPERTS, rows], F32, tag="bank", name="slot_sums")
+            for i in range(BANK_GROUPS):
+                g = bank_index * BANK_GROUPS + i
+                for t in range(PACK):
+                    nc.tensor.matmul(
+                        out=sums[:, t, :, i * GROUP_B : (i + 1) * GROUP_B],
+                        lhsT=token_pairs[bt][:, g, t:D:PACK],
+                        rhs=diagonal[:, :, g * GROUP_B : (g + 1) * GROUP_B],
+                        start=True,
+                        stop=True,
+                    )
+            nc.vector.tensor_copy(
+                out=grouped[bt][:, 0:PE_EXPERTS, bank_index * rows : (bank_index + 1) * rows, :],
+                in_=sums[:].rearrange("p t e b -> p e b t"),
+            )
+
+        pool_slots_bf = {}
+
+        def pool_slots(bt):
+            pool_slots_bf[bt] = keep.tile([P, POOL_EXPERTS, D], BF16, name="pool_slots%d" % bt)
+            sums = {}
+            for n in range(AGENTS):
+                for i in range(POOL_EXPERTS):
+                    weight = disp[:, bt, PE_EXPERTS + i, n : n + 1]
+                    if n == 0:
+                        sums[i] = pool_work.tile([P, D], F32, tag="sum%d" % i, bufs=1, name="sum%d" % i)
+                        nc.gpsimd.tensor_scalar(
+                            out=sums[i][:], in0=token_rows[bt][:, n, :], scalar1=weight, scalar2=0.0,
+                            op0=ALU.mult, op1=ALU.add,
+                        )
+                    else:
+                        product = pool_work.tile([P, D], F32, tag="product", name="product")
+                        nc.gpsimd.tensor_scalar(
+                            out=product[:], in0=token_rows[bt][:, n, :], scalar1=weight, scalar2=0.0,
+                            op0=ALU.mult, op1=ALU.add,
+                        )
+                        target = sums[i][:] if n < AGENTS - 1 else pool_slots_bf[bt][:, i, :]
+                        nc.gpsimd.tensor_tensor(out=target, in0=sums[i][:], in1=product[:], op=ALU.add)
+
+        def turn_pool_slots(bt):
+            for i in range(POOL_EXPERTS):
+                turned = psum.tile([P, PACK, P], BF16, tag="bank", name="turned_slots")
+                for t in range(PACK):
+                    nc.tensor.transpose(
+                        out=turned[:, t, :], in_=pool_slots_bf[bt][:, i, t:D:PACK], identity=ident[:]
+                    )
+                nc.vector.tensor_copy(
+                    out=grouped[bt][:, PE_EXPERTS + i, :, :], in_=turned[:].rearrange("p t b -> p b t")
+                )
+
+        def quantise_pair(bt, e):
+            pair = slice(e, e + 2)
+            nc.vector.quantize_mx(
+                out=codes[bt][:, pair, :].rearrange("p e b -> p (e b)").bitcast(FP8X4),
+                scales=slot_planes[bt][:, pair, :].rearrange("p e b -> p (e b)"),
+                in_=grouped[bt][:, pair, :, :].rearrange("p e b t -> p (e b t)"),
+            )
+
+        units = [(bt, e) for bt in range(B_TILES) for e in range(EXPERTS)]
+        rounds = [units[i : i + UNITS_PER_ROUND] for i in range(0, len(units), UNITS_PER_ROUND)]
+
+        def round_units(r):
+            return rounds[r] if 0 <= r < len(rounds) else []
+
+        centred = {}
+        curve = {}
+        squares = {}
+        log_var = {}
+        rstd = {}
+
+        def multiply_and_centre(r, j, unit):
+            bt, e = unit
+            h = work.tile([P, H], F32, tag="h", bufs=3, name="h")
+            h_sums = small.tile([P, 2], F32, tag="h_sums", name="h_sums")
+            for half in range(H // BANK):
+                cols = slice(half * BANK, (half + 1) * BANK)
+                sums = psum.tile([P, BANK], F32, tag="bank", name="layer_sums")
+                nc.tensor.matmul_mx(
+                    out=sums[:],
+                    lhsT=codes[bt][:, e, :].bitcast(FP8X4),
+                    lhsT_scale=slot_planes[bt][:, e, :],
+                    rhs=w_words[:, e, cols].bitcast(FP8X4),
+                    rhs_scale=w_planes[:, e, cols],
+                    start=True,
+                    stop=True,
+                )
+                nc.vector.scalar_tensor_tensor(
+                    out=h[:, cols], in0=sums[:], scalar=1.0, in1=bias_all[:, e, cols],
+                    op0=ALU.mult, op1=ALU.add, accum_out=h_sums[:, half : half + 1],
+                )
+            gain_bank = spread_vector(columns_gain, e * CHUNKS, "gain_bank")
+            minus_mean = small.tile([P, 1], F32, tag="minus_mean", name="minus_mean")
+            nc.vector.tensor_scalar(
+                out=minus_mean[:], in0=h_sums[:, 0:1], scalar1=h_sums[:, 1:2], scalar2=-1.0 / H,
+                op0=ALU.add, op1=ALU.mult,
+            )
+            unread = work.tile([P, H], BF16, tag="unread", bufs=2, name="unread")
+            nc.scalar.activation(
+                out=unread[:], in_=h[:], func=ACT.Square, bias=minus_mean[:], scale=1.0,
+                accum_out=squares[r][:, j : j + 1],
+            )
+            centred[unit] = work.tile([P, H], F32, tag="centred", name="centred")
+            nc.vector.scalar_tensor_tensor(
+                out=centred[unit][:], in0=h[:], scalar=minus_mean[:], in1=gain_bank[:],
+                op0=ALU.add, op1=ALU.mult,
+            )
+
+        def scale_shift_and_exp(r, j, unit):
+            bt, e = unit
+            shift_bank = spread_vector(columns_gain, (EXPERTS + e) * CHUNKS, "shift_bank")
+            v = centred[unit]
+            nc.vector.scalar_tensor_tensor(
+                out=v[:], in0=v[:], scalar=rstd[r][:, j : j + 1], in1=shift_bank[:],
+                op0=ALU.mult, op1=ALU.add,
+            )
+            curve[unit] = work.tile([P, H], F32, tag="curve", name="curve")
+            nc.scalar.activation(out=curve[unit][:], in_=v[:], func=ACT.Exp)
+
+        def finish(unit):
+            bt, e = unit
+            nc.scalar.activation(out=curve[unit][:], in_=curve[unit][:], func=ACT.Tanh)
+            nc.gpsimd.tensor_tensor(out=curve[unit][:], in0=curve[unit][:], in1=centred[unit][:], op=ALU.mult)
+            nc.sync.dma_start(out=out[bt * P : (bt + 1) * P, e, :], in_=curve[unit][:])
+
+        diagonal = {0: block_diagonal_weights(0)}
+        pool_slots(0)
+        for bank_index in range(ROUTE_BANKS):
+            tensor_slots(0, bank_index, diagonal[0])
+        for e in range(0, PE_EXPERTS, 2):
+            quantise_pair(0, e)
+        token_pairs[1] = load_token_pairs(1)
+        diagonal[1] = block_diagonal_weights(1)
+        token_rows[1] = load_token_rows(1)
+        pool_slots(1)
+
+        for r in range(-2, len(rounds)):
+            if round_units(r + 1):
+                rstd[r + 1] = small.tile([P, UNITS_PER_ROUND], F32, tag="rstd", name="rstd")
+                nc.scalar.activation(out=rstd[r + 1][:], in_=log_var[r + 1][:], func=ACT.Exp, scale=-0.5)
+            for unit in round_units(r):
+                finish(unit)
+            for j, unit in enumerate(round_units(r + 1)):
+                scale_shift_and_exp(r + 1, j, unit)
+
+            for unit in round_units(r + 1):
+                nc.scalar.activation(
+                    out=curve[unit][:], in_=curve[unit][:], func=ACT.Ln, bias=one_col[:], scale=1.0
+                )
+            if round_units(r + 2):
+                squares[r + 2] = small.tile([P, UNITS_PER_ROUND], F32, tag="squares", name="squares")
+            for j, unit in enumerate(round_units(r + 2)):
+                bt, e = unit
+                if r + 2 == 1:
+                    for bank_index in range(2 * j, 2 * j + 2):
+                        tensor_slots(1, bank_index, diagonal[1])
+                if e == PE_EXPERTS:
+                    turn_pool_slots(bt)
+                    quantise_pair(bt, PE_EXPERTS)
+                multiply_and_centre(r + 2, j, unit)
+            if r + 2 == 1:
+                for e in range(0, PE_EXPERTS, 2):
+                    quantise_pair(1, e)
+            if round_units(r + 2):
+                log_var[r + 2] = small.tile([P, UNITS_PER_ROUND], F32, tag="log_var", name="log_var")
+                nc.scalar.activation(
+                    out=log_var[r + 2][:], in_=squares[r + 2][:], func=ACT.Ln, bias=eps_col[:], scale=1.0 / H
+                )

@@ -26,7 +26,7 @@ B_TILES = BATCH_ROWS // P
 CHUNKS = H // P
 
 PE_EXPERTS = 6
-POOL_EXPERTS = EXPERTS - PE_EXPERTS
+ROW_EXPERTS = EXPERTS - PE_EXPERTS
 SPLIT = 2
 GROUP_B = P // (AGENTS * SPLIT)
 GROUPS = P // GROUP_B
@@ -111,6 +111,7 @@ def tile_softmoedynamics_pa_e_kernel(tc, tokens, logits, W1_words, W1_scales, b1
         )
         grown = keep.tile(wide, F32)
         nc.scalar.activation(out=grown[:], in_=shifted[:], func=ACT.Exp)
+        nc.scalar.activation(out=warm[:], in_=one_col[:], func=ACT.Ln)
         total = keep.tile([P, B_TILES, EXPERTS], F32)
         nc.vector.tensor_reduce(out=total[:], in_=grown[:], axis=AX.X, op=ALU.add)
         inverse = keep.tile([P, B_TILES, EXPERTS], F32)
@@ -143,7 +144,8 @@ def tile_softmoedynamics_pa_e_kernel(tc, tokens, logits, W1_words, W1_scales, b1
         columns_bias = rows_to_columns(rows_bias, "bias")
         columns_gain = rows_to_columns(rows_gain, "gain")
         bias_all = keep.tile([P, EXPERTS, H], BF16)
-        for e in range(EXPERTS):
+
+        def spread_bias(e):
             bias_bank = spread_vector(columns_bias, e * CHUNKS, "bias_bank")
             nc.scalar.copy(out=bias_all[:, e, :], in_=bias_bank[:])
 
@@ -170,10 +172,10 @@ def tile_softmoedynamics_pa_e_kernel(tc, tokens, logits, W1_words, W1_scales, b1
                     out=turned[:, e, :], in_=masked[:, e].rearrange("p b c -> p (b c)"), identity=ident[:]
                 )
             diagonal = keep.tile([P, PE_EXPERTS, P], BF16, name="diagonal%d" % bt)
-            nc.scalar.copy(out=diagonal[:], in_=turned[:])
+            nc.vector.tensor_copy(out=diagonal[:], in_=turned[:])
             return diagonal
 
-        def tensor_slots(bt, bank_index, diagonal):
+        def tensor_slots(bt, bank_index, diagonal, on_scalar):
             rows = BANK_GROUPS * GROUP_B
             sums = psum.tile([P, PACK, PE_EXPERTS, rows], F32, tag="bank", name="slot_sums")
             for i in range(BANK_GROUPS):
@@ -186,41 +188,51 @@ def tile_softmoedynamics_pa_e_kernel(tc, tokens, logits, W1_words, W1_scales, b1
                         start=True,
                         stop=True,
                     )
-            nc.vector.tensor_copy(
-                out=grouped[bt][:, 0:PE_EXPERTS, bank_index * rows : (bank_index + 1) * rows, :],
-                in_=sums[:].rearrange("p t e b -> p e b t"),
-            )
+            target = grouped[bt][:, 0:PE_EXPERTS, bank_index * rows : (bank_index + 1) * rows, :]
+            if on_scalar:
+                nc.scalar.copy(out=target, in_=sums[:].rearrange("p t e b -> p e b t"))
+            else:
+                nc.vector.tensor_copy(out=target, in_=sums[:].rearrange("p t e b -> p e b t"))
 
-        pool_slots_bf = {}
+        row_slots = {}
+        for bt in range(B_TILES):
+            row_slots[bt] = keep.tile([P, ROW_EXPERTS, D], BF16, name="row_slots%d" % bt)
 
-        def pool_slots(bt):
-            pool_slots_bf[bt] = keep.tile([P, POOL_EXPERTS, D], BF16, name="pool_slots%d" % bt)
-            sums = {}
+        def vector_row_slots(bt, i):
+            running = pool_work.tile([P, D], F32, tag="running", bufs=1, name="running")
             for n in range(AGENTS):
-                for i in range(POOL_EXPERTS):
-                    weight = disp[:, bt, PE_EXPERTS + i, n : n + 1]
+                weight = disp[:, bt, PE_EXPERTS + i, n : n + 1]
+                for cols in (slice(0, D // 2), slice(D // 2, D)):
                     if n == 0:
-                        sums[i] = pool_work.tile([P, D], F32, tag="sum%d" % i, bufs=1, name="sum%d" % i)
-                        nc.gpsimd.tensor_scalar(
-                            out=sums[i][:], in0=token_rows[bt][:, n, :], scalar1=weight, scalar2=0.0,
-                            op0=ALU.mult, op1=ALU.add,
+                        nc.vector.tensor_scalar(
+                            out=running[:, cols], in0=token_rows[bt][:, n, cols], scalar1=weight, scalar2=None,
+                            op0=ALU.mult,
                         )
                     else:
-                        product = pool_work.tile([P, D], F32, tag="product", name="product")
-                        nc.gpsimd.tensor_scalar(
-                            out=product[:], in0=token_rows[bt][:, n, :], scalar1=weight, scalar2=0.0,
+                        target = running[:, cols] if n < AGENTS - 1 else row_slots[bt][:, i, cols]
+                        nc.vector.scalar_tensor_tensor(
+                            out=target, in0=token_rows[bt][:, n, cols], scalar=weight, in1=running[:, cols],
                             op0=ALU.mult, op1=ALU.add,
                         )
-                        target = sums[i][:] if n < AGENTS - 1 else pool_slots_bf[bt][:, i, :]
-                        nc.gpsimd.tensor_tensor(out=target, in0=sums[i][:], in1=product[:], op=ALU.add)
 
-        def turn_pool_slots(bt):
-            for i in range(POOL_EXPERTS):
+        def pool_row_slots(bt, i):
+            running = pool_work.tile([P, D], F32, tag="pool_running", bufs=1, name="pool_running")
+            for n in range(AGENTS):
+                weight = disp[:, bt, PE_EXPERTS + i, n : n + 1]
+                product = running if n == 0 else pool_work.tile([P, D], F32, tag="product", name="product")
+                nc.gpsimd.tensor_scalar(
+                    out=product[:], in0=token_rows[bt][:, n, :], scalar1=weight, scalar2=0.0,
+                    op0=ALU.mult, op1=ALU.add,
+                )
+                if n > 0:
+                    target = running[:] if n < AGENTS - 1 else row_slots[bt][:, i, :]
+                    nc.gpsimd.tensor_tensor(out=target, in0=running[:], in1=product[:], op=ALU.add)
+
+        def turn_row_slots(bt):
+            for i in range(ROW_EXPERTS):
                 turned = psum.tile([P, PACK, P], BF16, tag="bank", name="turned_slots")
                 for t in range(PACK):
-                    nc.tensor.transpose(
-                        out=turned[:, t, :], in_=pool_slots_bf[bt][:, i, t:D:PACK], identity=ident[:]
-                    )
+                    nc.tensor.transpose(out=turned[:, t, :], in_=row_slots[bt][:, i, t:D:PACK], identity=ident[:])
                 nc.vector.tensor_copy(
                     out=grouped[bt][:, PE_EXPERTS + i, :, :], in_=turned[:].rearrange("p t b -> p b t")
                 )
@@ -235,6 +247,8 @@ def tile_softmoedynamics_pa_e_kernel(tc, tokens, logits, W1_words, W1_scales, b1
 
         units = [(bt, e) for bt in range(B_TILES) for e in range(EXPERTS)]
         rounds = [units[i : i + UNITS_PER_ROUND] for i in range(0, len(units), UNITS_PER_ROUND)]
+        last_round = len(rounds) - 1
+        pairs_per_round = UNITS_PER_ROUND // 2
 
         def round_units(r):
             return rounds[r] if 0 <= r < len(rounds) else []
@@ -242,13 +256,18 @@ def tile_softmoedynamics_pa_e_kernel(tc, tokens, logits, W1_words, W1_scales, b1
         centred = {}
         curve = {}
         squares = {}
+        moments = {}
         log_var = {}
         rstd = {}
 
         def multiply_and_centre(r, j, unit):
             bt, e = unit
-            h = work.tile([P, H], F32, tag="h", bufs=3, name="h")
-            h_sums = small.tile([P, 2], F32, tag="h_sums", name="h_sums")
+            on_scalar = j % 2 == 0
+            h = work.tile([P, H], F32, tag="h", bufs=4, name="h")
+            if on_scalar:
+                h_sums = small.tile([P, 2], F32, tag="h_sums", name="h_sums")
+            else:
+                h_stats = small.tile([P, 2, 6], F32, tag="h_stats", name="h_stats")
             for half in range(H // BANK):
                 cols = slice(half * BANK, (half + 1) * BANK)
                 sums = psum.tile([P, BANK], F32, tag="bank", name="layer_sums")
@@ -261,25 +280,34 @@ def tile_softmoedynamics_pa_e_kernel(tc, tokens, logits, W1_words, W1_scales, b1
                     start=True,
                     stop=True,
                 )
-                nc.vector.scalar_tensor_tensor(
-                    out=h[:, cols], in0=sums[:], scalar=1.0, in1=bias_all[:, e, cols],
-                    op0=ALU.mult, op1=ALU.add, accum_out=h_sums[:, half : half + 1],
-                )
+                if on_scalar:
+                    nc.vector.scalar_tensor_tensor(
+                        out=h[:, cols], in0=sums[:], scalar=1.0, in1=bias_all[:, e, cols],
+                        op0=ALU.mult, op1=ALU.add, accum_out=h_sums[:, half : half + 1],
+                    )
+                else:
+                    nc.vector.tensor_tensor(out=h[:, cols], in0=sums[:], in1=bias_all[:, e, cols], op=ALU.add)
+                    nc.vector.bn_stats(out=h_stats[:, half, :], in_=h[:, cols])
             gain_bank = spread_vector(columns_gain, e * CHUNKS, "gain_bank")
-            minus_mean = small.tile([P, 1], F32, tag="minus_mean", name="minus_mean")
-            nc.vector.tensor_scalar(
-                out=minus_mean[:], in0=h_sums[:, 0:1], scalar1=h_sums[:, 1:2], scalar2=-1.0 / H,
-                op0=ALU.add, op1=ALU.mult,
-            )
-            unread = work.tile([P, H], BF16, tag="unread", bufs=2, name="unread")
-            nc.scalar.activation(
-                out=unread[:], in_=h[:], func=ACT.Square, bias=minus_mean[:], scale=1.0,
-                accum_out=squares[r][:, j : j + 1],
-            )
+            if on_scalar:
+                mean_tile = small.tile([P, 1], F32, tag="mean", name="mean_tile")
+                mean = mean_tile[:]
+                nc.vector.tensor_scalar(
+                    out=mean, in0=h_sums[:, 0:1], scalar1=h_sums[:, 1:2], scalar2=1.0 / H,
+                    op0=ALU.add, op1=ALU.mult,
+                )
+                unread = work.tile([P, H], BF16, tag="unread", bufs=2, name="unread")
+                nc.scalar.activation(
+                    out=unread[:], in_=h[:], func=ACT.Square, bias=mean, scale=-1.0,
+                    accum_out=squares[r][:, j // 2 : j // 2 + 1],
+                )
+            else:
+                nc.vector.bn_aggr(out=moments[r][:, j // 2, :], in_=h_stats[:].rearrange("p a b -> p (a b)"))
+                mean = moments[r][:, j // 2, 0:1]
             centred[unit] = work.tile([P, H], F32, tag="centred", name="centred")
             nc.vector.scalar_tensor_tensor(
-                out=centred[unit][:], in0=h[:], scalar=minus_mean[:], in1=gain_bank[:],
-                op0=ALU.add, op1=ALU.mult,
+                out=centred[unit][:], in0=h[:], scalar=mean, in1=gain_bank[:],
+                op0=ALU.subtract, op1=ALU.mult,
             )
 
         def scale_shift_and_exp(r, j, unit):
@@ -293,52 +321,67 @@ def tile_softmoedynamics_pa_e_kernel(tc, tokens, logits, W1_words, W1_scales, b1
             curve[unit] = work.tile([P, H], F32, tag="curve", name="curve")
             nc.scalar.activation(out=curve[unit][:], in_=v[:], func=ACT.Exp)
 
-        def finish(unit):
+        def finish(r, unit):
             bt, e = unit
             nc.scalar.activation(out=curve[unit][:], in_=curve[unit][:], func=ACT.Tanh)
-            nc.gpsimd.tensor_tensor(out=curve[unit][:], in0=curve[unit][:], in1=centred[unit][:], op=ALU.mult)
+            engine = nc.vector if r == last_round else nc.gpsimd
+            engine.tensor_tensor(out=curve[unit][:], in0=curve[unit][:], in1=centred[unit][:], op=ALU.mult)
             nc.sync.dma_start(out=out[bt * P : (bt + 1) * P, e, :], in_=curve[unit][:])
 
+        for e in range(UNITS_PER_ROUND):
+            spread_bias(e)
         diagonal = {0: block_diagonal_weights(0)}
-        pool_slots(0)
+        vector_row_slots(0, 0)
+        pool_row_slots(0, 1)
         for bank_index in range(ROUTE_BANKS):
-            tensor_slots(0, bank_index, diagonal[0])
+            tensor_slots(0, bank_index, diagonal[0], True)
+        for e in range(UNITS_PER_ROUND, EXPERTS):
+            spread_bias(e)
         for e in range(0, PE_EXPERTS, 2):
             quantise_pair(0, e)
         token_pairs[1] = load_token_pairs(1)
         diagonal[1] = block_diagonal_weights(1)
         token_rows[1] = load_token_rows(1)
-        pool_slots(1)
+        for i in range(ROW_EXPERTS):
+            pool_row_slots(1, i)
 
         for r in range(-2, len(rounds)):
             if round_units(r + 1):
                 rstd[r + 1] = small.tile([P, UNITS_PER_ROUND], F32, tag="rstd", name="rstd")
                 nc.scalar.activation(out=rstd[r + 1][:], in_=log_var[r + 1][:], func=ACT.Exp, scale=-0.5)
             for unit in round_units(r):
-                finish(unit)
+                finish(r, unit)
             for j, unit in enumerate(round_units(r + 1)):
                 scale_shift_and_exp(r + 1, j, unit)
 
-            for unit in round_units(r + 1):
-                nc.scalar.activation(
-                    out=curve[unit][:], in_=curve[unit][:], func=ACT.Ln, bias=one_col[:], scale=1.0
-                )
             if round_units(r + 2):
-                squares[r + 2] = small.tile([P, UNITS_PER_ROUND], F32, tag="squares", name="squares")
-            for j, unit in enumerate(round_units(r + 2)):
-                bt, e = unit
-                if r + 2 == 1:
-                    for bank_index in range(2 * j, 2 * j + 2):
-                        tensor_slots(1, bank_index, diagonal[1])
-                if e == PE_EXPERTS:
-                    turn_pool_slots(bt)
-                    quantise_pair(bt, PE_EXPERTS)
-                multiply_and_centre(r + 2, j, unit)
+                squares[r + 2] = small.tile([P, pairs_per_round], F32, tag="squares", name="squares")
+                moments[r + 2] = small.tile([P, pairs_per_round, 2], F32, tag="moments", name="moments")
+            for j in range(UNITS_PER_ROUND):
+                if round_units(r + 2):
+                    bt, e = round_units(r + 2)[j]
+                    if r + 2 == 1:
+                        tensor_slots(1, 2 * j, diagonal[1], False)
+                        tensor_slots(1, 2 * j + 1, diagonal[1], True)
+                    if e == PE_EXPERTS:
+                        turn_row_slots(bt)
+                        quantise_pair(bt, PE_EXPERTS)
+                    multiply_and_centre(r + 2, j, (bt, e))
+                if round_units(r + 1):
+                    unit = round_units(r + 1)[j]
+                    nc.scalar.activation(
+                        out=curve[unit][:], in_=curve[unit][:], func=ACT.Ln, bias=one_col[:], scale=1.0
+                    )
             if r + 2 == 1:
                 for e in range(0, PE_EXPERTS, 2):
                     quantise_pair(1, e)
             if round_units(r + 2):
                 log_var[r + 2] = small.tile([P, UNITS_PER_ROUND], F32, tag="log_var", name="log_var")
                 nc.scalar.activation(
-                    out=log_var[r + 2][:], in_=squares[r + 2][:], func=ACT.Ln, bias=eps_col[:], scale=1.0 / H
+                    out=log_var[r + 2][:, 0:UNITS_PER_ROUND:2], in_=squares[r + 2][:], func=ACT.Ln,
+                    bias=eps_col[:], scale=1.0 / H,
+                )
+                nc.scalar.activation(
+                    out=log_var[r + 2][:, 1:UNITS_PER_ROUND:2], in_=moments[r + 2][:, :, 1], func=ACT.Ln,
+                    bias=eps_col[:], scale=1.0,
                 )

@@ -32,6 +32,7 @@ GROUP_B = P // (AGENTS * SPLIT)
 GROUPS = P // GROUP_B
 BANK_GROUPS = 2
 ROUTE_BANKS = GROUPS // BANK_GROUPS
+WARM_PASSES = 6
 UNITS_PER_ROUND = 4
 
 FLOPS = 2 * BATCH_ROWS * EXPERTS * D * H + 2 * BATCH_ROWS * AGENTS * EXPERTS * D
@@ -100,6 +101,27 @@ def tile_softmoedynamics_pa_e_kernel(tc, tokens, logits, W1_words, W1_scales, b1
         nc.vector.tensor_reduce(
             out=same_row[:], in_=ident[:].rearrange("p (g b) -> p b g", b=GROUP_B), axis=AX.X, op=ALU.add
         )
+
+        zeros = keep.tile([P, BANK * PACK], BF16, align_bytes=64)
+        nc.vector.memset(zeros[:], 0.0)
+        zero_words = keep.tile([P, BANK], U32, align_bytes=64)
+        zero_plane = keep.tile([P, BANK], U8, align_bytes=64)
+        nc.vector.quantize_mx(out=zero_words[:].bitcast(FP8X4), scales=zero_plane[:], in_=zeros[:])
+
+        def idle_pass():
+            unused = psum.tile([P, BANK], F32, tag="bank", name="unused")
+            nc.tensor.matmul_mx(
+                out=unused[:],
+                lhsT=zero_words[:, 0:P].bitcast(FP8X4),
+                lhsT_scale=zero_plane[:, 0:P],
+                rhs=zero_words[:].bitcast(FP8X4),
+                rhs_scale=zero_plane[:],
+                start=True,
+                stop=True,
+            )
+
+        for i in range(WARM_PASSES):
+            idle_pass()
 
         by_expert = logits_bf[:].rearrange("p t n e -> p t e n")
         wide = [P, B_TILES, EXPERTS, AGENTS]
@@ -188,6 +210,7 @@ def tile_softmoedynamics_pa_e_kernel(tc, tokens, logits, W1_words, W1_scales, b1
                         start=True,
                         stop=True,
                     )
+            idle_pass()
             target = grouped[bt][:, 0:PE_EXPERTS, bank_index * rows : (bank_index + 1) * rows, :]
             if on_scalar:
                 nc.scalar.copy(out=target, in_=sums[:].rearrange("p t e b -> p e b t"))

@@ -32,7 +32,6 @@ GROUP_B = P // (AGENTS * SPLIT)
 GROUPS = P // GROUP_B
 BANK_GROUPS = 2
 ROUTE_BANKS = GROUPS // BANK_GROUPS
-WARM_PASSES = 6
 UNITS_PER_ROUND = 4
 
 FLOPS = 2 * BATCH_ROWS * EXPERTS * D * H + 2 * BATCH_ROWS * AGENTS * EXPERTS * D
@@ -102,27 +101,6 @@ def tile_softmoedynamics_pa_e_kernel(tc, tokens, logits, W1_words, W1_scales, b1
             out=same_row[:], in_=ident[:].rearrange("p (g b) -> p b g", b=GROUP_B), axis=AX.X, op=ALU.add
         )
 
-        zeros = keep.tile([P, BANK * PACK], BF16, align_bytes=64)
-        nc.vector.memset(zeros[:], 0.0)
-        zero_words = keep.tile([P, BANK], U32, align_bytes=64)
-        zero_plane = keep.tile([P, BANK], U8, align_bytes=64)
-        nc.vector.quantize_mx(out=zero_words[:].bitcast(FP8X4), scales=zero_plane[:], in_=zeros[:])
-
-        def idle_pass():
-            unused = psum.tile([P, BANK], F32, tag="bank", name="unused")
-            nc.tensor.matmul_mx(
-                out=unused[:],
-                lhsT=zero_words[:, 0:P].bitcast(FP8X4),
-                lhsT_scale=zero_plane[:, 0:P],
-                rhs=zero_words[:].bitcast(FP8X4),
-                rhs_scale=zero_plane[:],
-                start=True,
-                stop=True,
-            )
-
-        for i in range(WARM_PASSES):
-            idle_pass()
-
         by_expert = logits_bf[:].rearrange("p t n e -> p t e n")
         wide = [P, B_TILES, EXPERTS, AGENTS]
         top = keep.tile([P, B_TILES, EXPERTS], F32)
@@ -179,7 +157,7 @@ def tile_softmoedynamics_pa_e_kernel(tc, tokens, logits, W1_words, W1_scales, b1
             codes[bt] = keep.tile([P, EXPERTS, P], U32, align_bytes=64, name="codes%d" % bt)
             slot_planes[bt] = keep.tile([P, EXPERTS, P], U8, align_bytes=64, name="slot_planes%d" % bt)
 
-        def block_diagonal_weights(bt):
+        def mask_weights(bt):
             shape = [P, PE_EXPERTS, GROUP_B, AGENTS * SPLIT]
             masked = keep.tile(shape, BF16, name="masked%d" % bt)
             nc.vector.tensor_tensor(
@@ -188,6 +166,9 @@ def tile_softmoedynamics_pa_e_kernel(tc, tokens, logits, W1_words, W1_scales, b1
                 in1=same_row[:].unsqueeze(1).unsqueeze(3).to_broadcast(shape),
                 op=ALU.mult,
             )
+            return masked
+
+        def block_diagonal_weights(bt, masked):
             turned = psum.tile([P, PE_EXPERTS, P], BF16, tag="bank", name="turned_weights")
             for e in range(PE_EXPERTS):
                 nc.tensor.transpose(
@@ -210,7 +191,6 @@ def tile_softmoedynamics_pa_e_kernel(tc, tokens, logits, W1_words, W1_scales, b1
                         start=True,
                         stop=True,
                     )
-            idle_pass()
             target = grouped[bt][:, 0:PE_EXPERTS, bank_index * rows : (bank_index + 1) * rows, :]
             if on_scalar:
                 nc.scalar.copy(out=target, in_=sums[:].rearrange("p t e b -> p e b t"))
@@ -271,11 +251,11 @@ def tile_softmoedynamics_pa_e_kernel(tc, tokens, logits, W1_words, W1_scales, b1
         units = [(bt, e) for bt in range(B_TILES) for e in range(EXPERTS)]
         rounds = [units[i : i + UNITS_PER_ROUND] for i in range(0, len(units), UNITS_PER_ROUND)]
         last_round = len(rounds) - 1
-        pairs_per_round = UNITS_PER_ROUND // 2
 
         def round_units(r):
             return rounds[r] if 0 <= r < len(rounds) else []
 
+        hidden = {}
         centred = {}
         curve = {}
         squares = {}
@@ -283,16 +263,18 @@ def tile_softmoedynamics_pa_e_kernel(tc, tokens, logits, W1_words, W1_scales, b1
         log_var = {}
         rstd = {}
 
-        def multiply_and_centre(r, j, unit):
+        def vector_takes_variance(unit):
             bt, e = unit
-            on_scalar = j % 2 == 0
-            h = work.tile([P, H], F32, tag="h", bufs=4, name="h")
-            if on_scalar:
+            return bt > 0 and e % 2 == 1
+
+        def multiply_and_sum(r, j, unit):
+            bt, e = unit
+            hidden[unit] = work.tile([P, H], F32, tag="hidden", bufs=UNITS_PER_ROUND, name="hidden")
+            h = hidden[unit]
+            halves = [slice(half * BANK, (half + 1) * BANK) for half in range(H // BANK)]
+            if not vector_takes_variance(unit):
                 h_sums = small.tile([P, 2], F32, tag="h_sums", name="h_sums")
-            else:
-                h_stats = small.tile([P, 2, 6], F32, tag="h_stats", name="h_stats")
-            for half in range(H // BANK):
-                cols = slice(half * BANK, (half + 1) * BANK)
+            for half, cols in enumerate(halves):
                 sums = psum.tile([P, BANK], F32, tag="bank", name="layer_sums")
                 nc.tensor.matmul_mx(
                     out=sums[:],
@@ -303,35 +285,51 @@ def tile_softmoedynamics_pa_e_kernel(tc, tokens, logits, W1_words, W1_scales, b1
                     start=True,
                     stop=True,
                 )
-                if on_scalar:
+                if vector_takes_variance(unit):
+                    nc.vector.tensor_tensor(out=h[:, cols], in0=sums[:], in1=bias_all[:, e, cols], op=ALU.add)
+                else:
                     nc.vector.scalar_tensor_tensor(
                         out=h[:, cols], in0=sums[:], scalar=1.0, in1=bias_all[:, e, cols],
                         op0=ALU.mult, op1=ALU.add, accum_out=h_sums[:, half : half + 1],
                     )
-                else:
-                    nc.vector.tensor_tensor(out=h[:, cols], in0=sums[:], in1=bias_all[:, e, cols], op=ALU.add)
+            if vector_takes_variance(unit):
+                h_stats = small.tile([P, 2, 6], F32, tag="h_stats", name="h_stats")
+                for half, cols in enumerate(halves):
                     nc.vector.bn_stats(out=h_stats[:, half, :], in_=h[:, cols])
-            gain_bank = spread_vector(columns_gain, e * CHUNKS, "gain_bank")
-            if on_scalar:
-                mean_tile = small.tile([P, 1], F32, tag="mean", name="mean_tile")
-                mean = mean_tile[:]
+                nc.vector.bn_aggr(out=moments[r][:, j, :], in_=h_stats[:].rearrange("p a b -> p (a b)"))
+            else:
                 nc.vector.tensor_scalar(
-                    out=mean, in0=h_sums[:, 0:1], scalar1=h_sums[:, 1:2], scalar2=1.0 / H,
+                    out=moments[r][:, j, 0:1], in0=h_sums[:, 0:1], scalar1=h_sums[:, 1:2], scalar2=1.0 / H,
                     op0=ALU.add, op1=ALU.mult,
                 )
                 unread = work.tile([P, H], BF16, tag="unread", bufs=2, name="unread")
                 nc.scalar.activation(
-                    out=unread[:], in_=h[:], func=ACT.Square, bias=mean, scale=-1.0,
-                    accum_out=squares[r][:, j // 2 : j // 2 + 1],
+                    out=unread[:], in_=h[:], func=ACT.Square, bias=moments[r][:, j, 0:1], scale=-1.0,
+                    accum_out=squares[r][:, j : j + 1],
                 )
-            else:
-                nc.vector.bn_aggr(out=moments[r][:, j // 2, :], in_=h_stats[:].rearrange("p a b -> p (a b)"))
-                mean = moments[r][:, j // 2, 0:1]
+
+        def centre_and_gain(r, j, unit):
+            bt, e = unit
+            gain_bank = spread_vector(columns_gain, e * CHUNKS, "gain_bank")
             centred[unit] = work.tile([P, H], F32, tag="centred", name="centred")
             nc.vector.scalar_tensor_tensor(
-                out=centred[unit][:], in0=h[:], scalar=mean, in1=gain_bank[:],
+                out=centred[unit][:], in0=hidden[unit][:], scalar=moments[r][:, j, 0:1], in1=gain_bank[:],
                 op0=ALU.subtract, op1=ALU.mult,
             )
+
+        def log_variance(r):
+            log_var[r] = small.tile([P, UNITS_PER_ROUND], F32, tag="log_var", name="log_var")
+            shared = any(vector_takes_variance(unit) for unit in rounds[r])
+            step = 2 if shared else 1
+            nc.scalar.activation(
+                out=log_var[r][:, 0:UNITS_PER_ROUND:step], in_=squares[r][:, 0:UNITS_PER_ROUND:step], func=ACT.Ln,
+                bias=eps_col[:], scale=1.0 / H,
+            )
+            if shared:
+                nc.scalar.activation(
+                    out=log_var[r][:, 1:UNITS_PER_ROUND:2], in_=moments[r][:, 1:UNITS_PER_ROUND:2, 1], func=ACT.Ln,
+                    bias=eps_col[:], scale=1.0,
+                )
 
         def scale_shift_and_exp(r, j, unit):
             bt, e = unit
@@ -353,7 +351,8 @@ def tile_softmoedynamics_pa_e_kernel(tc, tokens, logits, W1_words, W1_scales, b1
 
         for e in range(UNITS_PER_ROUND):
             spread_bias(e)
-        diagonal = {0: block_diagonal_weights(0)}
+        masked = [mask_weights(bt) for bt in range(B_TILES)]
+        diagonal = [block_diagonal_weights(bt, masked[bt]) for bt in range(B_TILES)]
         vector_row_slots(0, 0)
         pool_row_slots(0, 1)
         for bank_index in range(ROUTE_BANKS):
@@ -363,7 +362,6 @@ def tile_softmoedynamics_pa_e_kernel(tc, tokens, logits, W1_words, W1_scales, b1
         for e in range(0, PE_EXPERTS, 2):
             quantise_pair(0, e)
         token_pairs[1] = load_token_pairs(1)
-        diagonal[1] = block_diagonal_weights(1)
         token_rows[1] = load_token_rows(1)
         for i in range(ROW_EXPERTS):
             pool_row_slots(1, i)
@@ -378,8 +376,8 @@ def tile_softmoedynamics_pa_e_kernel(tc, tokens, logits, W1_words, W1_scales, b1
                 scale_shift_and_exp(r + 1, j, unit)
 
             if round_units(r + 2):
-                squares[r + 2] = small.tile([P, pairs_per_round], F32, tag="squares", name="squares")
-                moments[r + 2] = small.tile([P, pairs_per_round, 2], F32, tag="moments", name="moments")
+                squares[r + 2] = small.tile([P, UNITS_PER_ROUND], F32, tag="squares", name="squares")
+                moments[r + 2] = small.tile([P, UNITS_PER_ROUND, 2], F32, tag="moments", name="moments")
             for j in range(UNITS_PER_ROUND):
                 if round_units(r + 2):
                     bt, e = round_units(r + 2)[j]
@@ -389,22 +387,16 @@ def tile_softmoedynamics_pa_e_kernel(tc, tokens, logits, W1_words, W1_scales, b1
                     if e == PE_EXPERTS:
                         turn_row_slots(bt)
                         quantise_pair(bt, PE_EXPERTS)
-                    multiply_and_centre(r + 2, j, (bt, e))
+                    multiply_and_sum(r + 2, j, (bt, e))
                 if round_units(r + 1):
                     unit = round_units(r + 1)[j]
                     nc.scalar.activation(
                         out=curve[unit][:], in_=curve[unit][:], func=ACT.Ln, bias=one_col[:], scale=1.0
                     )
+            if round_units(r + 2):
+                log_variance(r + 2)
+            for j, unit in enumerate(round_units(r + 2)):
+                centre_and_gain(r + 2, j, unit)
             if r + 2 == 1:
                 for e in range(0, PE_EXPERTS, 2):
                     quantise_pair(1, e)
-            if round_units(r + 2):
-                log_var[r + 2] = small.tile([P, UNITS_PER_ROUND], F32, tag="log_var", name="log_var")
-                nc.scalar.activation(
-                    out=log_var[r + 2][:, 0:UNITS_PER_ROUND:2], in_=squares[r + 2][:], func=ACT.Ln,
-                    bias=eps_col[:], scale=1.0 / H,
-                )
-                nc.scalar.activation(
-                    out=log_var[r + 2][:, 1:UNITS_PER_ROUND:2], in_=moments[r + 2][:, :, 1], func=ACT.Ln,
-                    bias=eps_col[:], scale=1.0,
-                )

@@ -32,6 +32,7 @@ GROUP_B = P // (AGENTS * SPLIT)
 GROUPS = P // GROUP_B
 BANK_GROUPS = 2
 ROUTE_BANKS = GROUPS // BANK_GROUPS
+CENTRED_BUFS = 10
 UNITS_PER_ROUND = 4
 
 FLOPS = 2 * BATCH_ROWS * EXPERTS * D * H + 2 * BATCH_ROWS * AGENTS * EXPERTS * D
@@ -67,7 +68,7 @@ def tile_softmoedynamics_pa_e_kernel(tc, tokens, logits, W1_words, W1_scales, b1
             return pairs
 
         def load_token_rows(bt):
-            by_row = token_pool.tile([P, AGENTS, D], BF16, tag="by_row", name="by_row%d" % bt)
+            by_row = token_pool.tile([P, AGENTS, D], BF16, tag="by_row", bufs=B_TILES, name="by_row%d" % bt)
             nc.sync.dma_start(out=by_row[:], in_=tokens[bt * P : (bt + 1) * P])
             return by_row
 
@@ -87,6 +88,8 @@ def tile_softmoedynamics_pa_e_kernel(tc, tokens, logits, W1_words, W1_scales, b1
                 out=w_words[:, e, :].bitcast(I32),
                 in_=W1_words[e].rearrange("p n t -> p (n t)").bitcast(I32),
             )
+            if e == UNITS_PER_ROUND - 1:
+                token_rows[1] = load_token_rows(1)
 
         ident = keep.tile([P, P], BF16)
         make_identity(nc, ident[:])
@@ -100,29 +103,6 @@ def tile_softmoedynamics_pa_e_kernel(tc, tokens, logits, W1_words, W1_scales, b1
         nc.vector.tensor_reduce(
             out=same_row[:], in_=ident[:].rearrange("p (g b) -> p b g", b=GROUP_B), axis=AX.X, op=ALU.add
         )
-
-        by_expert = logits_bf[:].rearrange("p t n e -> p t e n")
-        wide = [P, B_TILES, EXPERTS, AGENTS]
-        top = keep.tile([P, B_TILES, EXPERTS], F32)
-        nc.vector.tensor_reduce(out=top[:], in_=by_expert, axis=AX.X, op=ALU.max)
-        shifted = keep.tile(wide, F32)
-        nc.vector.tensor_tensor(
-            out=shifted[:], in0=by_expert, in1=top[:].unsqueeze(3).to_broadcast(wide), op=ALU.subtract
-        )
-        grown = keep.tile(wide, F32)
-        nc.scalar.activation(out=grown[:], in_=shifted[:], func=ACT.Exp)
-        nc.scalar.activation(out=warm[:], in_=one_col[:], func=ACT.Ln)
-        total = keep.tile([P, B_TILES, EXPERTS], F32)
-        nc.vector.tensor_reduce(out=total[:], in_=grown[:], axis=AX.X, op=ALU.add)
-        inverse = keep.tile([P, B_TILES, EXPERTS], F32)
-        nc.vector.reciprocal(out=inverse[:], in_=total[:])
-        disp = keep.tile(wide, F32)
-        nc.vector.tensor_tensor(
-            out=disp[:], in0=grown[:], in1=inverse[:].unsqueeze(3).to_broadcast(wide), op=ALU.mult
-        )
-        hi_lo = keep.tile(wide + [SPLIT], BF16)
-        nc.vector.tensor_copy(out=hi_lo[:, :, :, :, 0], in_=disp[:])
-        nc.vector.tensor_tensor(out=hi_lo[:, :, :, :, 1], in0=disp[:], in1=hi_lo[:, :, :, :, 0], op=ALU.subtract)
 
         def rows_to_columns(rows, name):
             turned = psum.tile([P, P], BF16, tag="bank", name="turned_" + name)
@@ -148,6 +128,28 @@ def tile_softmoedynamics_pa_e_kernel(tc, tokens, logits, W1_words, W1_scales, b1
         def spread_bias(e):
             bias_bank = spread_vector(columns_bias, e * CHUNKS, "bias_bank")
             nc.scalar.copy(out=bias_all[:, e, :], in_=bias_bank[:])
+
+        by_expert = logits_bf[:].rearrange("p t n e -> p t e n")
+        wide = [P, B_TILES, EXPERTS, AGENTS]
+        top = keep.tile([P, B_TILES, EXPERTS], F32)
+        nc.vector.tensor_reduce(out=top[:], in_=by_expert, axis=AX.X, op=ALU.max)
+        shifted = keep.tile(wide, F32)
+        nc.vector.tensor_tensor(
+            out=shifted[:], in0=by_expert, in1=top[:].unsqueeze(3).to_broadcast(wide), op=ALU.subtract
+        )
+        grown = keep.tile(wide, F32)
+        nc.scalar.activation(out=grown[:], in_=shifted[:], func=ACT.Exp)
+        total = keep.tile([P, B_TILES, EXPERTS], F32)
+        nc.vector.tensor_reduce(out=total[:], in_=grown[:], axis=AX.X, op=ALU.add)
+        inverse = keep.tile([P, B_TILES, EXPERTS], F32)
+        nc.vector.reciprocal(out=inverse[:], in_=total[:])
+        disp = keep.tile(wide, F32)
+        nc.vector.tensor_tensor(
+            out=disp[:], in0=grown[:], in1=inverse[:].unsqueeze(3).to_broadcast(wide), op=ALU.mult
+        )
+        hi_lo = keep.tile(wide + [SPLIT], BF16)
+        nc.vector.tensor_copy(out=hi_lo[:, :, :, :, 0], in_=disp[:])
+        nc.vector.tensor_tensor(out=hi_lo[:, :, :, :, 1], in0=disp[:], in1=hi_lo[:, :, :, :, 0], op=ALU.subtract)
 
         grouped = {}
         codes = {}
@@ -311,7 +313,7 @@ def tile_softmoedynamics_pa_e_kernel(tc, tokens, logits, W1_words, W1_scales, b1
         def centre_and_gain(r, j, unit):
             bt, e = unit
             gain_bank = spread_vector(columns_gain, e * CHUNKS, "gain_bank")
-            centred[unit] = work.tile([P, H], F32, tag="centred", name="centred")
+            centred[unit] = work.tile([P, H], F32, tag="centred", bufs=CENTRED_BUFS, name="centred")
             nc.vector.scalar_tensor_tensor(
                 out=centred[unit][:], in0=hidden[unit][:], scalar=moments[r][:, j, 0:1], in1=gain_bank[:],
                 op0=ALU.subtract, op1=ALU.mult,
@@ -349,7 +351,7 @@ def tile_softmoedynamics_pa_e_kernel(tc, tokens, logits, W1_words, W1_scales, b1
             engine.tensor_tensor(out=curve[unit][:], in0=curve[unit][:], in1=centred[unit][:], op=ALU.mult)
             nc.sync.dma_start(out=out[bt * P : (bt + 1) * P, e, :], in_=curve[unit][:])
 
-        for e in range(UNITS_PER_ROUND):
+        for e in range(EXPERTS):
             spread_bias(e)
         masked = [mask_weights(bt) for bt in range(B_TILES)]
         diagonal = [block_diagonal_weights(bt, masked[bt]) for bt in range(B_TILES)]
@@ -357,12 +359,10 @@ def tile_softmoedynamics_pa_e_kernel(tc, tokens, logits, W1_words, W1_scales, b1
         pool_row_slots(0, 1)
         for bank_index in range(ROUTE_BANKS):
             tensor_slots(0, bank_index, diagonal[0], True)
-        for e in range(UNITS_PER_ROUND, EXPERTS):
-            spread_bias(e)
+        nc.scalar.activation(out=warm[:], in_=one_col[:], func=ACT.Ln)
         for e in range(0, PE_EXPERTS, 2):
             quantise_pair(0, e)
         token_pairs[1] = load_token_pairs(1)
-        token_rows[1] = load_token_rows(1)
         for i in range(ROW_EXPERTS):
             pool_row_slots(1, i)
 

@@ -220,9 +220,13 @@ def tile_softmoedynamics_pa_e_kernel(tc, tokens, logits, W1_words, W1_scales, b1
                             op0=ALU.mult, op1=ALU.add,
                         )
 
-        def pool_row_slots(bt, i):
-            running = pool_work.tile([P, D], F32, tag="pool_running", bufs=1, name="pool_running")
-            for n in range(AGENTS):
+        pool_running = {}
+
+        def pool_row_slots(bt, i, agents):
+            if 0 in agents:
+                pool_running[(bt, i)] = pool_work.tile([P, D], F32, tag="pool_running", bufs=1, name="pool_running")
+            running = pool_running[(bt, i)]
+            for n in agents:
                 weight = disp[:, bt, PE_EXPERTS + i, n : n + 1]
                 product = running if n == 0 else pool_work.tile([P, D], F32, tag="product", name="product")
                 nc.gpsimd.tensor_scalar(
@@ -267,7 +271,7 @@ def tile_softmoedynamics_pa_e_kernel(tc, tokens, logits, W1_words, W1_scales, b1
 
         def vector_takes_variance(unit):
             bt, e = unit
-            return bt > 0 and e % 2 == 1
+            return units.index(unit) >= UNITS_PER_ROUND and e % 2 == 1
 
         def multiply_and_sum(r, j, unit):
             bt, e = unit
@@ -346,32 +350,43 @@ def tile_softmoedynamics_pa_e_kernel(tc, tokens, logits, W1_words, W1_scales, b1
 
         def finish(r, unit):
             bt, e = unit
-            nc.scalar.activation(out=curve[unit][:], in_=curve[unit][:], func=ACT.Tanh)
             engine = nc.vector if r == last_round else nc.gpsimd
-            engine.tensor_tensor(out=curve[unit][:], in0=curve[unit][:], in1=centred[unit][:], op=ALU.mult)
-            nc.sync.dma_start(out=out[bt * P : (bt + 1) * P, e, :], in_=curve[unit][:])
+            pieces = 2 if r == last_round else 1
+            width = H // pieces
+            for piece in range(pieces):
+                cols = slice(piece * width, (piece + 1) * width)
+                nc.scalar.activation(out=curve[unit][:, cols], in_=curve[unit][:, cols], func=ACT.Tanh)
+                engine.tensor_tensor(
+                    out=curve[unit][:, cols], in0=curve[unit][:, cols], in1=centred[unit][:, cols], op=ALU.mult
+                )
+                nc.sync.dma_start(out=out[bt * P : (bt + 1) * P, e, cols], in_=curve[unit][:, cols])
 
-        for e in range(EXPERTS):
+        for e in range(UNITS_PER_ROUND):
             spread_bias(e)
         masked = [mask_weights(bt) for bt in range(B_TILES)]
         diagonal = [block_diagonal_weights(bt, masked[bt]) for bt in range(B_TILES)]
         vector_row_slots(0, 0)
-        pool_row_slots(0, 1)
+        pool_row_slots(0, 1, range(AGENTS))
         for bank_index in range(ROUTE_BANKS):
             tensor_slots(0, bank_index, diagonal[0], True)
         nc.scalar.activation(out=warm[:], in_=one_col[:], func=ACT.Ln)
         for e in range(0, PE_EXPERTS, 2):
             quantise_pair(0, e)
         token_pairs[1] = load_token_pairs(1)
-        for i in range(ROW_EXPERTS):
-            pool_row_slots(1, i)
+        pool_row_slots(1, 0, range(AGENTS))
+        pool_row_slots(1, 1, range(AGENTS // 2))
 
         for r in range(-2, len(rounds)):
             if round_units(r + 1):
                 rstd[r + 1] = small.tile([P, UNITS_PER_ROUND], F32, tag="rstd", name="rstd")
                 nc.scalar.activation(out=rstd[r + 1][:], in_=log_var[r + 1][:], func=ACT.Exp, scale=-0.5)
+            if r + 1 == 0:
+                for e in range(UNITS_PER_ROUND, EXPERTS):
+                    spread_bias(e)
             for unit in round_units(r):
                 finish(r, unit)
+            if r == 0:
+                pool_row_slots(1, 1, range(AGENTS // 2, AGENTS))
             for j, unit in enumerate(round_units(r + 1)):
                 scale_shift_and_exp(r + 1, j, unit)
 

@@ -22,6 +22,7 @@ H = 1024
 EPS = 1e-5
 PACK = 4
 BANK = 512
+PLANES = 4
 B_TILES = BATCH_ROWS // P
 CHUNKS = H // P
 
@@ -75,13 +76,14 @@ def tile_softmoedynamics_pa_e_kernel(tc, tokens, logits, W1_words, W1_scales, b1
         token_pairs = {0: load_token_pairs(0)}
         token_rows = {0: load_token_rows(0)}
 
-        w_planes = keep.tile([P, EXPERTS, H], U8, align_bytes=64)
-        nc.vector.memset(w_planes[:].rearrange("p e n -> p (e n)").bitcast(I32), 0)
-        for quad in range(4):
-            nc.sync.dma_start(
-                out=w_planes[32 * quad : 32 * quad + 4, :, :].bitcast(I32),
-                in_=W1_scales[:, 4 * quad : 4 * quad + 4, :].rearrange("g r n -> r g n").bitcast(I32),
-            )
+        w_planes = keep.tile([P, EXPERTS // PLANES, H], U8, align_bytes=64)
+        nc.vector.memset(w_planes[:].rearrange("p s n -> p (s n)").bitcast(I32), 0)
+        for s in range(EXPERTS // PLANES):
+            for quad in range(4):
+                nc.sync.dma_start(
+                    out=w_planes[32 * quad : 32 * quad + 4 * PLANES, s, :].bitcast(I32),
+                    in_=W1_scales[s * PLANES : (s + 1) * PLANES, 4 * quad : 4 * quad + 4, :].bitcast(I32),
+                )
         w_words = keep.tile([P, EXPERTS, H], U32, align_bytes=64)
         for e in range(EXPERTS):
             nc.sync.dma_start(
@@ -287,7 +289,7 @@ def tile_softmoedynamics_pa_e_kernel(tc, tokens, logits, W1_words, W1_scales, b1
                     lhsT=codes[bt][:, e, :].bitcast(FP8X4),
                     lhsT_scale=slot_planes[bt][:, e, :],
                     rhs=w_words[:, e, cols].bitcast(FP8X4),
-                    rhs_scale=w_planes[:, e, cols],
+                    rhs_scale=w_planes[4 * (e % PLANES) : P, e // PLANES, cols],
                     start=True,
                     stop=True,
                 )

@@ -63,10 +63,13 @@ def tile_softmoedynamics_pa_e_kernel(tc, tokens, logits, W1_words, W1_scales, b1
 
         def load_token_pairs(bt):
             pairs = token_pool.tile([P, GROUPS, D], BF16, tag="pairs", name="pairs%d" % bt)
+            load_groups(bt, pairs, slice(0, GROUPS // 2))
+            return pairs
+
+        def load_groups(bt, pairs, some):
             rows = tokens[bt * P : (bt + 1) * P].rearrange("(g b) n d -> (b n) g d", b=GROUP_B)
             for s in range(SPLIT):
-                nc.sync.dma_start(out=pairs[s:P:SPLIT, :, :], in_=rows)
-            return pairs
+                nc.sync.dma_start(out=pairs[s:P:SPLIT, some, :], in_=rows[:, some, :])
 
         def load_token_rows(bt):
             by_row = token_pool.tile([P, AGENTS, D], BF16, tag="by_row", bufs=B_TILES, name="by_row%d" % bt)
@@ -75,6 +78,7 @@ def tile_softmoedynamics_pa_e_kernel(tc, tokens, logits, W1_words, W1_scales, b1
 
         token_pairs = {0: load_token_pairs(0)}
         token_rows = {0: load_token_rows(0)}
+        load_groups(0, token_pairs[0], slice(GROUPS // 2, GROUPS))
 
         w_planes = keep.tile([P, EXPERTS // PLANES, H], U8, align_bytes=64)
         nc.vector.memset(w_planes[:].rearrange("p s n -> p (s n)").bitcast(I32), 0)
@@ -375,6 +379,7 @@ def tile_softmoedynamics_pa_e_kernel(tc, tokens, logits, W1_words, W1_scales, b1
         for e in range(0, PE_EXPERTS, 2):
             quantise_pair(0, e)
         token_pairs[1] = load_token_pairs(1)
+        load_groups(1, token_pairs[1], slice(GROUPS // 2, GROUPS))
         pool_row_slots(1, 0, range(AGENTS))
         pool_row_slots(1, 1, range(AGENTS // 2))
 

@@ -58,8 +58,6 @@ def tile_softmoedynamics_pa_e_kernel(tc, tokens, logits, W1_words, W1_scales, b1
         half_rows = EXPERTS * CHUNKS
         nc.vector.memset(rows_bias[half_rows:P, :], 0.0)
         nc.sync.dma_start(out=rows_bias[0:half_rows, :], in_=b1.rearrange("e (c p) -> (e c) p", p=P))
-        nc.sync.dma_start(out=rows_gain[0:half_rows, :], in_=g1.rearrange("e (c p) -> (e c) p", p=P))
-        nc.sync.dma_start(out=rows_gain[half_rows:P, :], in_=be1.rearrange("e (c p) -> (e c) p", p=P))
 
         def load_token_pairs(bt):
             pairs = token_pool.tile([P, GROUPS, D], BF16, tag="pairs", name="pairs%d" % bt)
@@ -82,19 +80,26 @@ def tile_softmoedynamics_pa_e_kernel(tc, tokens, logits, W1_words, W1_scales, b1
 
         w_planes = keep.tile([P, EXPERTS // PLANES, H], U8, align_bytes=64)
         nc.vector.memset(w_planes[:].rearrange("p s n -> p (s n)").bitcast(I32), 0)
-        for s in range(EXPERTS // PLANES):
+
+        def load_planes(s):
             for quad in range(4):
                 nc.sync.dma_start(
                     out=w_planes[32 * quad : 32 * quad + 4 * PLANES, s, :].bitcast(I32),
                     in_=W1_scales[s * PLANES : (s + 1) * PLANES, 4 * quad : 4 * quad + 4, :].bitcast(I32),
                 )
+
+        load_planes(0)
         w_words = keep.tile([P, EXPERTS, H], U32, align_bytes=64)
         for e in range(EXPERTS):
             nc.sync.dma_start(
                 out=w_words[:, e, :].bitcast(I32),
                 in_=W1_words[e].rearrange("p n t -> p (n t)").bitcast(I32),
             )
+            if e == 0:
+                nc.sync.dma_start(out=rows_gain[0:half_rows, :], in_=g1.rearrange("e (c p) -> (e c) p", p=P))
+                nc.sync.dma_start(out=rows_gain[half_rows:P, :], in_=be1.rearrange("e (c p) -> (e c) p", p=P))
             if e == UNITS_PER_ROUND - 1:
+                load_planes(1)
                 token_rows[1] = load_token_rows(1)
 
         ident = keep.tile([P, P], BF16)
@@ -128,7 +133,6 @@ def tile_softmoedynamics_pa_e_kernel(tc, tokens, logits, W1_words, W1_scales, b1
             return bank
 
         columns_bias = rows_to_columns(rows_bias, "bias")
-        columns_gain = rows_to_columns(rows_gain, "gain")
         bias_all = keep.tile([P, EXPERTS, H], BF16)
 
         def spread_bias(e):
@@ -375,6 +379,7 @@ def tile_softmoedynamics_pa_e_kernel(tc, tokens, logits, W1_words, W1_scales, b1
         pool_row_slots(0, 1, range(AGENTS))
         for bank_index in range(ROUTE_BANKS):
             tensor_slots(0, bank_index, diagonal[0], True)
+        columns_gain = rows_to_columns(rows_gain, "gain")
         nc.scalar.activation(out=warm[:], in_=one_col[:], func=ACT.Ln)
         for e in range(0, PE_EXPERTS, 2):
             quantise_pair(0, e)

@@ -33,6 +33,7 @@ GROUP_B = P // (AGENTS * SPLIT)
 GROUPS = P // GROUP_B
 BANK_GROUPS = 2
 ROUTE_BANKS = GROUPS // BANK_GROUPS
+VECTOR_COLUMNS = 768
 CENTRED_BUFS = 10
 UNITS_PER_ROUND = 4
 
@@ -267,6 +268,7 @@ def tile_softmoedynamics_pa_e_kernel(tc, tokens, logits, W1_words, W1_scales, b1
         units = [(bt, e) for bt in range(B_TILES) for e in range(EXPERTS)]
         rounds = [units[i : i + UNITS_PER_ROUND] for i in range(0, len(units), UNITS_PER_ROUND)]
         last_round = len(rounds) - 1
+        vector_unit = rounds[last_round][0]
 
         def round_units(r):
             return rounds[r] if 0 <= r < len(rounds) else []
@@ -358,13 +360,33 @@ def tile_softmoedynamics_pa_e_kernel(tc, tokens, logits, W1_words, W1_scales, b1
             curve[unit] = work.tile([P, H], F32, tag="curve", name="curve")
             nc.scalar.activation(out=curve[unit][:], in_=v[:], func=ACT.Exp)
 
+        def vector_mish(unit):
+            bt, e = unit
+            u = curve[unit]
+            v = centred[unit]
+            for cols in [slice(i * VECTOR_COLUMNS // 1, (i + 1) * VECTOR_COLUMNS // 1) for i in range(1)]:
+                nc.vector.scalar_tensor_tensor(
+                    out=u[:, cols], in0=u[:, cols], scalar=2.0, in1=u[:, cols], op0=ALU.add, op1=ALU.mult
+                )
+                nc.vector.tensor_scalar(
+                    out=u[:, cols], in0=u[:, cols], scalar1=-0.5, scalar2=-1.0, op0=ALU.mult, op1=ALU.add
+                )
+                nc.vector.reciprocal(out=u[:, cols], in_=u[:, cols])
+                nc.vector.scalar_tensor_tensor(
+                    out=u[:, cols], in0=u[:, cols], scalar=1.0, in1=v[:, cols], op0=ALU.add, op1=ALU.mult
+                )
+                nc.sync.dma_start(out=out[bt * P : (bt + 1) * P, e, cols], in_=u[:, cols])
+
         def finish(r, unit):
             bt, e = unit
             engine = nc.vector if r == last_round else nc.gpsimd
             pieces = 2 if r == last_round else 1
-            width = H // pieces
+            first = VECTOR_COLUMNS if unit == vector_unit else 0
+            if unit == vector_unit:
+                pieces = 1
+            width = (H - first) // pieces
             for piece in range(pieces):
-                cols = slice(piece * width, (piece + 1) * width)
+                cols = slice(first + piece * width, first + (piece + 1) * width)
                 nc.scalar.activation(out=curve[unit][:, cols], in_=curve[unit][:, cols], func=ACT.Tanh)
                 engine.tensor_tensor(
                     out=curve[unit][:, cols], in0=curve[unit][:, cols], in1=centred[unit][:, cols], op=ALU.mult
@@ -417,8 +439,12 @@ def tile_softmoedynamics_pa_e_kernel(tc, tokens, logits, W1_words, W1_scales, b1
                     multiply_and_sum(r + 2, j, (bt, e))
                 if round_units(r + 1):
                     unit = round_units(r + 1)[j]
+                    first = 0
+                    if unit == vector_unit:
+                        vector_mish(unit)
+                        first = VECTOR_COLUMNS
                     nc.scalar.activation(
-                        out=curve[unit][:], in_=curve[unit][:], func=ACT.Ln, bias=one_col[:], scale=1.0
+                        out=curve[unit][:, first:H], in_=curve[unit][:, first:H], func=ACT.Ln, bias=one_col[:], scale=1.0
                     )
             if round_units(r + 2):
                 log_variance(r + 2)

@@ -235,18 +235,22 @@ def tile_softmoedynamics_pa_e_kernel(tc, tokens, logits, W1_words, W1_scales, b1
 
         def pool_row_slots(bt, i, agents):
             if 0 in agents:
-                pool_running[(bt, i)] = pool_work.tile([P, D], F32, tag="pool_running", bufs=1, name="pool_running")
+                pool_running[(bt, i)] = pool_work.tile([P, 2, D], F32, tag="pool_running", bufs=1, name="pool_running")
             running = pool_running[(bt, i)]
-            for n in agents:
-                weight = disp[:, bt, PE_EXPERTS + i, n : n + 1]
-                product = running if n == 0 else pool_work.tile([P, D], F32, tag="product", name="product")
-                nc.gpsimd.tensor_scalar(
-                    out=product[:], in0=token_rows[bt][:, n, :], scalar1=weight, scalar2=0.0,
-                    op0=ALU.mult, op1=ALU.add,
+            for first in agents[::2]:
+                pair = running if first == 0 else pool_work.tile([P, 2, D], F32, tag="product", name="product")
+                for a in range(2):
+                    weight = disp[:, bt, PE_EXPERTS + i, first + a : first + a + 1]
+                    nc.gpsimd.tensor_scalar(
+                        out=pair[:, a, :], in0=token_rows[bt][:, first + a, :], scalar1=weight, scalar2=0.0,
+                        op0=ALU.mult, op1=ALU.add,
+                    )
+                if first > 0:
+                    nc.gpsimd.tensor_tensor(out=running[:], in0=running[:], in1=pair[:], op=ALU.add)
+            if AGENTS - 1 in agents:
+                nc.gpsimd.tensor_tensor(
+                    out=row_slots[bt][:, i, :], in0=running[:, 0, :], in1=running[:, 1, :], op=ALU.add
                 )
-                if n > 0:
-                    target = running[:] if n < AGENTS - 1 else row_slots[bt][:, i, :]
-                    nc.gpsimd.tensor_tensor(out=target, in0=running[:], in1=product[:], op=ALU.add)
 
         def turn_row_slots(bt):
             for i in range(ROW_EXPERTS):
@@ -282,8 +286,14 @@ def tile_softmoedynamics_pa_e_kernel(tc, tokens, logits, W1_words, W1_scales, b1
         rstd = {}
 
         def vector_takes_variance(unit):
-            bt, e = unit
-            return units.index(unit) >= UNITS_PER_ROUND and e % 2 == 1
+            place = units.index(unit)
+            return place >= UNITS_PER_ROUND and place % 2 == 1 or place in (10,)
+
+        late = []
+
+        def run_late():
+            while late:
+                late.pop(0)()
 
         def multiply_and_sum(r, j, unit):
             bt, e = unit
@@ -310,21 +320,27 @@ def tile_softmoedynamics_pa_e_kernel(tc, tokens, logits, W1_words, W1_scales, b1
                         out=h[:, cols], in0=sums[:], scalar=1.0, in1=bias_all[:, e, cols],
                         op0=ALU.mult, op1=ALU.add, accum_out=h_sums[:, half : half + 1],
                     )
+                run_late()
             if vector_takes_variance(unit):
                 h_stats = small.tile([P, 2, 6], F32, tag="h_stats", name="h_stats")
                 for half, cols in enumerate(halves):
                     nc.vector.bn_stats(out=h_stats[:, half, :], in_=h[:, cols])
-                nc.vector.bn_aggr(out=moments[r][:, j, :], in_=h_stats[:].rearrange("p a b -> p (a b)"))
+                late.append(lambda: nc.vector.bn_aggr(
+                    out=moments[r][:, j, :], in_=h_stats[:].rearrange("p a b -> p (a b)")
+                ))
             else:
-                nc.vector.tensor_scalar(
-                    out=moments[r][:, j, 0:1], in0=h_sums[:, 0:1], scalar1=h_sums[:, 1:2], scalar2=1.0 / H,
-                    op0=ALU.add, op1=ALU.mult,
-                )
-                unread = work.tile([P, H], BF16, tag="unread", bufs=2, name="unread")
-                nc.scalar.activation(
-                    out=unread[:], in_=h[:], func=ACT.Square, bias=moments[r][:, j, 0:1], scale=-1.0,
-                    accum_out=squares[r][:, j : j + 1],
-                )
+                late.append(lambda: mean_and_squares(r, j, unit, h_sums))
+
+        def mean_and_squares(r, j, unit, h_sums):
+            nc.vector.tensor_scalar(
+                out=moments[r][:, j, 0:1], in0=h_sums[:, 0:1], scalar1=h_sums[:, 1:2], scalar2=1.0 / H,
+                op0=ALU.add, op1=ALU.mult,
+            )
+            unread = work.tile([P, H], BF16, tag="unread", bufs=2, name="unread")
+            nc.scalar.activation(
+                out=unread[:], in_=hidden[unit][:], func=ACT.Square, bias=moments[r][:, j, 0:1], scale=-1.0,
+                accum_out=squares[r][:, j : j + 1],
+            )
 
         def centre_and_gain(r, j, unit):
             bt, e = unit
@@ -337,17 +353,15 @@ def tile_softmoedynamics_pa_e_kernel(tc, tokens, logits, W1_words, W1_scales, b1
 
         def log_variance(r):
             log_var[r] = small.tile([P, UNITS_PER_ROUND], F32, tag="log_var", name="log_var")
-            shared = any(vector_takes_variance(unit) for unit in rounds[r])
-            step = 2 if shared else 1
-            nc.scalar.activation(
-                out=log_var[r][:, 0:UNITS_PER_ROUND:step], in_=squares[r][:, 0:UNITS_PER_ROUND:step], func=ACT.Ln,
-                bias=eps_col[:], scale=1.0 / H,
-            )
-            if shared:
-                nc.scalar.activation(
-                    out=log_var[r][:, 1:UNITS_PER_ROUND:2], in_=moments[r][:, 1:UNITS_PER_ROUND:2, 1], func=ACT.Ln,
-                    bias=eps_col[:], scale=1.0,
-                )
+            by_vector = [j for j, unit in enumerate(rounds[r]) if vector_takes_variance(unit)]
+            by_scalar = [j for j in range(UNITS_PER_ROUND) if j not in by_vector]
+            for columns, source, scale in ((by_scalar, squares[r], 1.0 / H), (by_vector, moments[r][:, :, 1], 1.0)):
+                if columns:
+                    step = columns[1] - columns[0] if len(columns) > 1 else 1
+                    some = slice(columns[0], columns[-1] + 1, step)
+                    nc.scalar.activation(
+                        out=log_var[r][:, some], in_=source[:, some], func=ACT.Ln, bias=eps_col[:], scale=scale
+                    )
 
         def scale_shift_and_exp(r, j, unit):
             bt, e = unit
@@ -433,7 +447,7 @@ def tile_softmoedynamics_pa_e_kernel(tc, tokens, logits, W1_words, W1_scales, b1
                     if r + 2 == 1:
                         tensor_slots(1, 2 * j, diagonal[1], False)
                         tensor_slots(1, 2 * j + 1, diagonal[1], True)
-                    if e == PE_EXPERTS:
+                    if e == (PE_EXPERTS - 1 if bt == 0 else PE_EXPERTS):
                         turn_row_slots(bt)
                         quantise_pair(bt, PE_EXPERTS)
                     multiply_and_sum(r + 2, j, (bt, e))
@@ -446,10 +460,11 @@ def tile_softmoedynamics_pa_e_kernel(tc, tokens, logits, W1_words, W1_scales, b1
                     nc.scalar.activation(
                         out=curve[unit][:, first:H], in_=curve[unit][:, first:H], func=ACT.Ln, bias=one_col[:], scale=1.0
                     )
-            if round_units(r + 2):
-                log_variance(r + 2)
             for j, unit in enumerate(round_units(r + 2)):
                 centre_and_gain(r + 2, j, unit)
+                if j == 0:
+                    run_late()
+                    log_variance(r + 2)
             if r + 2 == 1:
                 for e in range(0, PE_EXPERTS, 2):
                     quantise_pair(1, e)

@@ -33,7 +33,6 @@ GROUP_B = P // (AGENTS * SPLIT)
 GROUPS = P // GROUP_B
 BANK_GROUPS = 2
 ROUTE_BANKS = GROUPS // BANK_GROUPS
-VECTOR_COLUMNS = 768
 CENTRED_BUFS = 10
 UNITS_PER_ROUND = 4
 
@@ -272,8 +271,6 @@ def tile_softmoedynamics_pa_e_kernel(tc, tokens, logits, W1_words, W1_scales, b1
         units = [(bt, e) for bt in range(B_TILES) for e in range(EXPERTS)]
         rounds = [units[i : i + UNITS_PER_ROUND] for i in range(0, len(units), UNITS_PER_ROUND)]
         last_round = len(rounds) - 1
-        vector_unit = rounds[last_round][0]
-
         def round_units(r):
             return rounds[r] if 0 <= r < len(rounds) else []
 
@@ -367,45 +364,46 @@ def tile_softmoedynamics_pa_e_kernel(tc, tokens, logits, W1_words, W1_scales, b1
             bt, e = unit
             shift_bank = spread_vector(columns_gain, (EXPERTS + e) * CHUNKS, "shift_bank")
             v = centred[unit]
+            last = r == last_round
             nc.vector.scalar_tensor_tensor(
                 out=v[:], in0=v[:], scalar=rstd[r][:, j : j + 1], in1=shift_bank[:],
-                op0=ALU.mult, op1=ALU.add,
+                op0=ALU.mult, op1=ALU.subtract if last else ALU.add,
             )
             curve[unit] = work.tile([P, H], F32, tag="curve", name="curve")
-            nc.scalar.activation(out=curve[unit][:], in_=v[:], func=ACT.Exp)
+            nc.scalar.activation(out=curve[unit][:], in_=v[:], func=ACT.Exp, scale=-1.0 if last else 1.0)
 
-        def vector_mish(unit):
-            bt, e = unit
+        def first_product(unit):
             u = curve[unit]
-            v = centred[unit]
-            for cols in [slice(i * VECTOR_COLUMNS // 1, (i + 1) * VECTOR_COLUMNS // 1) for i in range(1)]:
+            nc.vector.scalar_tensor_tensor(
+                out=u[:], in0=u[:], scalar=2.0, in1=u[:], op0=ALU.add, op1=ALU.mult
+            )
+
+        def root(unit):
+            nc.scalar.activation(
+                out=curve[unit][:], in_=curve[unit][:], func=ACT.Abs_reciprocal_sqrt, bias=one_col[:], scale=0.5
+            )
+
+        def square_of_root(j, unit):
+            c = curve[unit]
+            if j >= UNITS_PER_ROUND // 2:
+                nc.scalar.activation(out=c[:], in_=c[:], func=ACT.Square)
+            else:
+                nc.vector.tensor_tensor(out=c[:], in0=c[:], in1=c[:], op=ALU.mult)
+
+        def last_product(unit):
+            bt, e = unit
+            for cols in (slice(0, H // 2), slice(H // 2, H)):
                 nc.vector.scalar_tensor_tensor(
-                    out=u[:, cols], in0=u[:, cols], scalar=2.0, in1=u[:, cols], op0=ALU.add, op1=ALU.mult
+                    out=curve[unit][:, cols], in0=curve[unit][:, cols], scalar=1.0, in1=centred[unit][:, cols],
+                    op0=ALU.subtract, op1=ALU.mult,
                 )
-                nc.vector.tensor_scalar(
-                    out=u[:, cols], in0=u[:, cols], scalar1=-0.5, scalar2=-1.0, op0=ALU.mult, op1=ALU.add
-                )
-                nc.vector.reciprocal(out=u[:, cols], in_=u[:, cols])
-                nc.vector.scalar_tensor_tensor(
-                    out=u[:, cols], in0=u[:, cols], scalar=1.0, in1=v[:, cols], op0=ALU.add, op1=ALU.mult
-                )
-                nc.sync.dma_start(out=out[bt * P : (bt + 1) * P, e, cols], in_=u[:, cols])
+                nc.sync.dma_start(out=out[bt * P : (bt + 1) * P, e, cols], in_=curve[unit][:, cols])
 
         def finish(r, unit):
             bt, e = unit
-            engine = nc.vector if r == last_round else nc.gpsimd
-            pieces = 2 if r == last_round else 1
-            first = VECTOR_COLUMNS if unit == vector_unit else 0
-            if unit == vector_unit:
-                pieces = 1
-            width = (H - first) // pieces
-            for piece in range(pieces):
-                cols = slice(first + piece * width, first + (piece + 1) * width)
-                nc.scalar.activation(out=curve[unit][:, cols], in_=curve[unit][:, cols], func=ACT.Tanh)
-                engine.tensor_tensor(
-                    out=curve[unit][:, cols], in0=curve[unit][:, cols], in1=centred[unit][:, cols], op=ALU.mult
-                )
-                nc.sync.dma_start(out=out[bt * P : (bt + 1) * P, e, cols], in_=curve[unit][:, cols])
+            nc.scalar.activation(out=curve[unit][:], in_=curve[unit][:], func=ACT.Tanh)
+            nc.gpsimd.tensor_tensor(out=curve[unit][:], in0=curve[unit][:], in1=centred[unit][:], op=ALU.mult)
+            nc.sync.dma_start(out=out[bt * P : (bt + 1) * P, e, :], in_=curve[unit][:])
 
         for e in range(UNITS_PER_ROUND):
             spread_bias(e)
@@ -431,12 +429,25 @@ def tile_softmoedynamics_pa_e_kernel(tc, tokens, logits, W1_words, W1_scales, b1
             if r + 1 == 0:
                 for e in range(UNITS_PER_ROUND, EXPERTS):
                     spread_bias(e)
-            for unit in round_units(r):
-                finish(r, unit)
+            for j, unit in enumerate(round_units(r)):
+                if r == last_round:
+                    square_of_root(j, unit)
+                else:
+                    finish(r, unit)
+            if r == last_round:
+                for unit in round_units(r):
+                    last_product(unit)
             if r == 0:
                 pool_row_slots(1, 1, range(AGENTS // 2, AGENTS))
+            if r + 1 == last_round:
+                nc.vector.tensor_scalar(
+                    out=rstd[r + 1][:], in0=rstd[r + 1][:], scalar1=-1.0, scalar2=None, op0=ALU.mult
+                )
             for j, unit in enumerate(round_units(r + 1)):
                 scale_shift_and_exp(r + 1, j, unit)
+            if r + 1 == last_round:
+                for unit in round_units(r + 1):
+                    first_product(unit)
 
             if round_units(r + 2):
                 squares[r + 2] = small.tile([P, UNITS_PER_ROUND], F32, tag="squares", name="squares")
@@ -453,13 +464,12 @@ def tile_softmoedynamics_pa_e_kernel(tc, tokens, logits, W1_words, W1_scales, b1
                     multiply_and_sum(r + 2, j, (bt, e))
                 if round_units(r + 1):
                     unit = round_units(r + 1)[j]
-                    first = 0
-                    if unit == vector_unit:
-                        vector_mish(unit)
-                        first = VECTOR_COLUMNS
-                    nc.scalar.activation(
-                        out=curve[unit][:, first:H], in_=curve[unit][:, first:H], func=ACT.Ln, bias=one_col[:], scale=1.0
-                    )
+                    if r + 1 == last_round:
+                        root(unit)
+                    else:
+                        nc.scalar.activation(
+                            out=curve[unit][:], in_=curve[unit][:], func=ACT.Ln, bias=one_col[:], scale=1.0
+                        )
             for j, unit in enumerate(round_units(r + 2)):
                 centre_and_gain(r + 2, j, unit)
                 if j == 0:

@@ -169,10 +169,10 @@ def tile_softmoedynamics_pa_e_kernel(tc, tokens, logits, W1_words, W1_scales, b1
             codes[bt] = keep.tile([P, EXPERTS, P], U32, align_bytes=64, name="codes%d" % bt)
             slot_planes[bt] = keep.tile([P, EXPERTS, P], U8, align_bytes=64, name="slot_planes%d" % bt)
 
-        def mask_weights(bt):
+        def mask_weights(bt, engine):
             shape = [P, PE_EXPERTS, GROUP_B, AGENTS * SPLIT]
             masked = keep.tile(shape, BF16, name="masked%d" % bt)
-            nc.vector.tensor_tensor(
+            engine.tensor_tensor(
                 out=masked[:],
                 in0=hi_lo[:, bt, 0:PE_EXPERTS].rearrange("p e n s -> p e (n s)").unsqueeze(2).to_broadcast(shape),
                 in1=same_row[:].unsqueeze(1).unsqueeze(3).to_broadcast(shape),
@@ -187,7 +187,10 @@ def tile_softmoedynamics_pa_e_kernel(tc, tokens, logits, W1_words, W1_scales, b1
                     out=turned[:, e, :], in_=masked[:, e].rearrange("p b c -> p (b c)"), identity=ident[:]
                 )
             diagonal = keep.tile([P, PE_EXPERTS, P], BF16, name="diagonal%d" % bt)
-            nc.vector.tensor_copy(out=diagonal[:], in_=turned[:])
+            if bt == 0:
+                nc.vector.tensor_copy(out=diagonal[:], in_=turned[:])
+            else:
+                nc.scalar.copy(out=diagonal[:], in_=turned[:])
             return diagonal
 
         def tensor_slots(bt, bank_index, diagonal, on_scalar):
@@ -284,7 +287,7 @@ def tile_softmoedynamics_pa_e_kernel(tc, tokens, logits, W1_words, W1_scales, b1
 
         def vector_takes_variance(unit):
             place = units.index(unit)
-            return place >= UNITS_PER_ROUND and place % 2 == 1 or place in (10,)
+            return place >= UNITS_PER_ROUND and place % 2 == 1 or place in (10, 14)
 
         late = []
 
@@ -292,14 +295,13 @@ def tile_softmoedynamics_pa_e_kernel(tc, tokens, logits, W1_words, W1_scales, b1
             while late:
                 late.pop(0)()
 
-        def multiply_and_sum(r, j, unit):
+        layer_sums = {}
+        halves = [slice(half * BANK, (half + 1) * BANK) for half in range(H // BANK)]
+
+        def multiply(unit):
             bt, e = unit
-            hidden[unit] = work.tile([P, H], F32, tag="hidden", bufs=UNITS_PER_ROUND, name="hidden")
-            h = hidden[unit]
-            halves = [slice(half * BANK, (half + 1) * BANK) for half in range(H // BANK)]
-            if not vector_takes_variance(unit):
-                h_sums = small.tile([P, 2], F32, tag="h_sums", name="h_sums")
-            for half, cols in enumerate(halves):
+            layer_sums[unit] = []
+            for cols in halves:
                 sums = psum.tile([P, BANK], F32, tag="bank", name="layer_sums")
                 nc.tensor.matmul_mx(
                     out=sums[:],
@@ -310,6 +312,16 @@ def tile_softmoedynamics_pa_e_kernel(tc, tokens, logits, W1_words, W1_scales, b1
                     start=True,
                     stop=True,
                 )
+                layer_sums[unit].append(sums)
+
+        def add_bias_and_sum(r, j, unit):
+            bt, e = unit
+            hidden[unit] = work.tile([P, H], F32, tag="hidden", bufs=UNITS_PER_ROUND, name="hidden")
+            h = hidden[unit]
+            if not vector_takes_variance(unit):
+                h_sums = small.tile([P, 2], F32, tag="h_sums", name="h_sums")
+            for half, cols in enumerate(halves):
+                sums = layer_sums[unit][half]
                 if vector_takes_variance(unit):
                     nc.vector.tensor_tensor(out=h[:, cols], in0=sums[:], in1=bias_all[:, e, cols], op=ALU.add)
                 else:
@@ -400,19 +412,28 @@ def tile_softmoedynamics_pa_e_kernel(tc, tokens, logits, W1_words, W1_scales, b1
                 nc.sync.dma_start(out=out[bt * P : (bt + 1) * P, e, cols], in_=curve[unit][:, cols])
 
         def finish(r, unit):
-            bt, e = unit
             nc.scalar.activation(out=curve[unit][:], in_=curve[unit][:], func=ACT.Tanh)
-            nc.gpsimd.tensor_tensor(out=curve[unit][:], in0=curve[unit][:], in1=centred[unit][:], op=ALU.mult)
+            if not vector_takes_product(unit):
+                product(nc.gpsimd, unit)
+
+        def vector_takes_product(unit):
+            return unit in rounds[last_round - 1][UNITS_PER_ROUND // 2 :]
+
+        def product(engine, unit):
+            bt, e = unit
+            engine.tensor_tensor(out=curve[unit][:], in0=curve[unit][:], in1=centred[unit][:], op=ALU.mult)
             nc.sync.dma_start(out=out[bt * P : (bt + 1) * P, e, :], in_=curve[unit][:])
 
         for e in range(UNITS_PER_ROUND):
             spread_bias(e)
-        masked = [mask_weights(bt) for bt in range(B_TILES)]
-        diagonal = [block_diagonal_weights(bt, masked[bt]) for bt in range(B_TILES)]
+        masked = [mask_weights(0, nc.vector), mask_weights(1, nc.gpsimd)]
+        diagonal = [block_diagonal_weights(0, masked[0])]
         vector_row_slots(0, 0)
         pool_row_slots(0, 1, range(AGENTS))
         for bank_index in range(ROUTE_BANKS):
             tensor_slots(0, bank_index, diagonal[0], True)
+        for e in range(UNITS_PER_ROUND, 6):
+            spread_bias(e)
         columns_gain = rows_to_columns(rows_gain, "gain")
         nc.scalar.activation(out=warm[:], in_=one_col[:], func=ACT.Ln)
         for e in range(0, PE_EXPERTS, 2):
@@ -427,7 +448,8 @@ def tile_softmoedynamics_pa_e_kernel(tc, tokens, logits, W1_words, W1_scales, b1
                 rstd[r + 1] = small.tile([P, UNITS_PER_ROUND], F32, tag="rstd", name="rstd")
                 nc.scalar.activation(out=rstd[r + 1][:], in_=log_var[r + 1][:], func=ACT.Exp, scale=-0.5)
             if r + 1 == 0:
-                for e in range(UNITS_PER_ROUND, EXPERTS):
+                diagonal.append(block_diagonal_weights(1, masked[1]))
+                for e in range(6, EXPERTS):
                     spread_bias(e)
             for j, unit in enumerate(round_units(r)):
                 if r == last_round:
@@ -448,6 +470,9 @@ def tile_softmoedynamics_pa_e_kernel(tc, tokens, logits, W1_words, W1_scales, b1
             if r + 1 == last_round:
                 for unit in round_units(r + 1):
                     first_product(unit)
+                for unit in round_units(r):
+                    if vector_takes_product(unit):
+                        product(nc.vector, unit)
 
             if round_units(r + 2):
                 squares[r + 2] = small.tile([P, UNITS_PER_ROUND], F32, tag="squares", name="squares")
@@ -455,13 +480,14 @@ def tile_softmoedynamics_pa_e_kernel(tc, tokens, logits, W1_words, W1_scales, b1
             for j in range(UNITS_PER_ROUND):
                 if round_units(r + 2):
                     bt, e = round_units(r + 2)[j]
+                    multiply((bt, e))
+                    if e == PE_EXPERTS - 1:
+                        turn_row_slots(bt)
+                        quantise_pair(bt, PE_EXPERTS)
+                    add_bias_and_sum(r + 2, j, (bt, e))
                     if r + 2 == 1:
                         tensor_slots(1, 2 * j, diagonal[1], False)
                         tensor_slots(1, 2 * j + 1, diagonal[1], True)
-                    if e == (PE_EXPERTS - 1 if bt == 0 else PE_EXPERTS):
-                        turn_row_slots(bt)
-                        quantise_pair(bt, PE_EXPERTS)
-                    multiply_and_sum(r + 2, j, (bt, e))
                 if round_units(r + 1):
                     unit = round_units(r + 1)[j]
                     if r + 1 == last_round:

@@ -74,8 +74,8 @@ def tile_softmoedynamics_pa_e_kernel(tc, tokens, logits, W1_words, W1_scales, b1
             nc.sync.dma_start(out=by_row[:], in_=tokens[bt * P : (bt + 1) * P])
             return by_row
 
-        token_pairs = {0: load_token_pairs(0)}
         token_rows = {0: load_token_rows(0)}
+        token_pairs = {0: load_token_pairs(0)}
         load_groups(0, token_pairs[0], slice(GROUPS // 2, GROUPS))
 
         w_planes = keep.tile([P, EXPERTS // PLANES, H], U8, align_bytes=64)
@@ -90,11 +90,15 @@ def tile_softmoedynamics_pa_e_kernel(tc, tokens, logits, W1_words, W1_scales, b1
 
         load_planes(0)
         w_words = keep.tile([P, EXPERTS, H], U32, align_bytes=64)
-        for e in range(EXPERTS):
+
+        def load_weight(e):
             nc.sync.dma_start(
                 out=w_words[:, e, :].bitcast(I32),
                 in_=W1_words[e].rearrange("p n t -> p (n t)").bitcast(I32),
             )
+
+        for e in range(6):
+            load_weight(e)
             if e == 0:
                 nc.sync.dma_start(out=rows_gain[0:half_rows, :], in_=g1.rearrange("e (c p) -> (e c) p", p=P))
                 nc.sync.dma_start(out=rows_gain[half_rows:P, :], in_=be1.rearrange("e (c p) -> (e c) p", p=P))
@@ -113,6 +117,10 @@ def tile_softmoedynamics_pa_e_kernel(tc, tokens, logits, W1_words, W1_scales, b1
         same_row = keep.tile([P, GROUP_B], F32)
         nc.vector.tensor_reduce(
             out=same_row[:], in_=ident[:].rearrange("p (g b) -> p b g", b=GROUP_B), axis=AX.X, op=ALU.add
+        )
+        pair_row = keep.tile([P, GROUP_B, AGENTS * SPLIT], BF16)
+        nc.vector.tensor_copy(
+            out=pair_row[:], in_=same_row[:].unsqueeze(2).to_broadcast([P, GROUP_B, AGENTS * SPLIT])
         )
 
         def rows_to_columns(rows, name):
@@ -175,7 +183,7 @@ def tile_softmoedynamics_pa_e_kernel(tc, tokens, logits, W1_words, W1_scales, b1
             engine.tensor_tensor(
                 out=masked[:],
                 in0=hi_lo[:, bt, 0:PE_EXPERTS].rearrange("p e n s -> p e (n s)").unsqueeze(2).to_broadcast(shape),
-                in1=same_row[:].unsqueeze(1).unsqueeze(3).to_broadcast(shape),
+                in1=pair_row[:].unsqueeze(1).to_broadcast(shape),
                 op=ALU.mult,
             )
             return masked
@@ -216,9 +224,13 @@ def tile_softmoedynamics_pa_e_kernel(tc, tokens, logits, W1_words, W1_scales, b1
         for bt in range(B_TILES):
             row_slots[bt] = keep.tile([P, ROW_EXPERTS, D], BF16, name="row_slots%d" % bt)
 
-        def vector_row_slots(bt, i):
-            running = pool_work.tile([P, D], F32, tag="running", bufs=1, name="running")
-            for n in range(AGENTS):
+        running_rows = {}
+
+        def vector_row_slots(bt, i, agents):
+            if 0 in agents:
+                running_rows[bt] = pool_work.tile([P, D], F32, tag="running", bufs=1, name="running")
+            running = running_rows[bt]
+            for n in agents:
                 weight = disp[:, bt, PE_EXPERTS + i, n : n + 1]
                 for cols in (slice(0, D // 2), slice(D // 2, D)):
                     if n == 0:
@@ -427,11 +439,12 @@ def tile_softmoedynamics_pa_e_kernel(tc, tokens, logits, W1_words, W1_scales, b1
         for e in range(UNITS_PER_ROUND):
             spread_bias(e)
         masked = [mask_weights(0, nc.vector), mask_weights(1, nc.gpsimd)]
+        vector_row_slots(0, 0, range(2))
         diagonal = [block_diagonal_weights(0, masked[0])]
-        vector_row_slots(0, 0)
+        vector_row_slots(0, 0, range(2, AGENTS))
         pool_row_slots(0, 1, range(AGENTS))
         for bank_index in range(ROUTE_BANKS):
-            tensor_slots(0, bank_index, diagonal[0], True)
+            tensor_slots(0, bank_index, diagonal[0], bank_index not in (5, 7))
         for e in range(UNITS_PER_ROUND, 6):
             spread_bias(e)
         columns_gain = rows_to_columns(rows_gain, "gain")
@@ -440,6 +453,8 @@ def tile_softmoedynamics_pa_e_kernel(tc, tokens, logits, W1_words, W1_scales, b1
             quantise_pair(0, e)
         token_pairs[1] = load_token_pairs(1)
         load_groups(1, token_pairs[1], slice(GROUPS // 2, GROUPS))
+        for e in range(6, EXPERTS):
+            load_weight(e)
         pool_row_slots(1, 0, range(AGENTS))
         pool_row_slots(1, 1, range(AGENTS // 2))
 

@@ -75,8 +75,6 @@ def tile_softmoedynamics_pa_e_kernel(tc, tokens, logits, W1_words, W1_scales, b1
             return by_row
 
         token_rows = {0: load_token_rows(0)}
-        token_pairs = {0: load_token_pairs(0)}
-        load_groups(0, token_pairs[0], slice(GROUPS // 2, GROUPS))
 
         w_planes = keep.tile([P, EXPERTS // PLANES, H], U8, align_bytes=64)
         nc.vector.memset(w_planes[:].rearrange("p s n -> p (s n)").bitcast(I32), 0)
@@ -89,6 +87,8 @@ def tile_softmoedynamics_pa_e_kernel(tc, tokens, logits, W1_words, W1_scales, b1
                 )
 
         load_planes(0)
+        token_pairs = {0: load_token_pairs(0)}
+        load_groups(0, token_pairs[0], slice(GROUPS // 2, GROUPS))
         w_words = keep.tile([P, EXPERTS, H], U32, align_bytes=64)
 
         def load_weight(e):
@@ -108,6 +108,8 @@ def tile_softmoedynamics_pa_e_kernel(tc, tokens, logits, W1_words, W1_scales, b1
 
         ident = keep.tile([P, P], BF16)
         make_identity(nc, ident[:])
+        ident_f = keep.tile([P, P], F32)
+        make_identity(nc, ident_f[:])
         eps_col = keep.tile([P, 1], F32)
         nc.vector.memset(eps_col[:], EPS)
         one_col = keep.tile([P, 1], F32)
@@ -267,13 +269,17 @@ def tile_softmoedynamics_pa_e_kernel(tc, tokens, logits, W1_words, W1_scales, b1
                 )
 
         def turn_row_slots(bt):
+            turned = psum.tile([P, ROW_EXPERTS, P, PACK // 2], F32, tag="bank", name="turned_slots")
             for i in range(ROW_EXPERTS):
-                turned = psum.tile([P, PACK, P], BF16, tag="bank", name="turned_slots")
-                for t in range(PACK):
-                    nc.tensor.transpose(out=turned[:, t, :], in_=row_slots[bt][:, i, t:D:PACK], identity=ident[:])
-                nc.vector.tensor_copy(
-                    out=grouped[bt][:, PE_EXPERTS + i, :, :], in_=turned[:].rearrange("p t b -> p b t")
-                )
+                words = row_slots[bt][:, i, :].bitcast(F32)
+                for s in range(PACK // 2):
+                    nc.tensor.transpose(
+                        out=turned[:, i, :, s], in_=words[:, s : D // 2 : PACK // 2], identity=ident_f[:]
+                    )
+            nc.vector.tensor_copy(
+                out=grouped[bt][:, PE_EXPERTS:EXPERTS, :, :].rearrange("p e b t -> p (e b t)").bitcast(F32),
+                in_=turned[:].rearrange("p e b s -> p (e b s)"),
+            )
 
         def quantise_pair(bt, e):
             pair = slice(e, e + 2)

from contextlib import ExitStack

import concourse.mybir as mybir
from concourse.masks import make_identity

F32 = mybir.dt.float32
BF16 = mybir.dt.bfloat16
I32 = mybir.dt.int32
U32 = mybir.dt.uint32
U8 = mybir.dt.uint8
FP8X4 = mybir.dt.float8_e4m3fn_x4
ALU = mybir.AluOpType
ACT = mybir.ActivationFunctionType
AX = mybir.AxisListType

P = 128
BATCH_ROWS = 256
AGENTS = 8
EXPERTS = 8
D = 512
H = 1024
EPS = 1e-5
PACK = 4
BANK = 512
PLANES = 4
B_TILES = BATCH_ROWS // P
CHUNKS = H // P

PE_EXPERTS = 6
ROW_EXPERTS = EXPERTS - PE_EXPERTS
SPLIT = 2
GROUP_B = P // (AGENTS * SPLIT)
GROUPS = P // GROUP_B
BANK_GROUPS = 2
ROUTE_BANKS = GROUPS // BANK_GROUPS
CENTRED_BUFS = 10
UNITS_PER_ROUND = 4

FLOPS = 2 * BATCH_ROWS * EXPERTS * D * H + 2 * BATCH_ROWS * AGENTS * EXPERTS * D


def tile_softmoedynamics_pa_e_kernel(tc, tokens, logits, W1_words, W1_scales, b1, g1, be1, out):
    nc = tc.nc
    with ExitStack() as ctx:
        ctx.enter_context(tc.manual_schedule())
        keep = ctx.enter_context(tc.tile_pool(name="keep", bufs=1))
        token_pool = ctx.enter_context(tc.tile_pool(name="token_pool", bufs=1))
        pool_work = ctx.enter_context(tc.tile_pool(name="pool_work", bufs=2))
        work = ctx.enter_context(tc.tile_pool(name="work", bufs=8))
        small = ctx.enter_context(tc.tile_pool(name="small", bufs=8))
        psum = ctx.enter_context(tc.psum_pool(name="psum", bufs=8))

        logits_bf = keep.tile([P, B_TILES, AGENTS, EXPERTS], BF16)
        nc.sync.dma_start(out=logits_bf[:], in_=logits.rearrange("(t p) n e -> p t n e", p=P))

        rows_gain = keep.tile([P, P], BF16)
        rows_bias = keep.tile([P, P], BF16)
        half_rows = EXPERTS * CHUNKS
        nc.vector.memset(rows_bias[half_rows:P, :], 0.0)
        nc.sync.dma_start(out=rows_bias[0:half_rows, :], in_=b1.rearrange("e (c p) -> (e c) p", p=P))

        def load_token_pairs(bt):
            pairs = token_pool.tile([P, GROUPS, D], BF16, tag="pairs", name="pairs%d" % bt)
            load_groups(bt, pairs, slice(0, GROUPS // 2))
            return pairs

        def load_groups(bt, pairs, some):
            rows = tokens[bt * P : (bt + 1) * P].rearrange("(g b) n d -> (b n) g d", b=GROUP_B)
            for s in range(SPLIT):
                nc.sync.dma_start(out=pairs[s:P:SPLIT, some, :], in_=rows[:, some, :])

        def load_token_rows(bt):
            by_row = token_pool.tile([P, AGENTS, D], BF16, tag="by_row", bufs=B_TILES, name="by_row%d" % bt)
            nc.sync.dma_start(out=by_row[:], in_=tokens[bt * P : (bt + 1) * P])
            return by_row

        token_rows = {0: load_token_rows(0)}

        w_planes = keep.tile([P, EXPERTS // PLANES, H], U8, align_bytes=64)
        nc.vector.memset(w_planes[:].rearrange("p s n -> p (s n)").bitcast(I32), 0)

        def load_planes(s):
            for quad in range(4):
                nc.sync.dma_start(
                    out=w_planes[32 * quad : 32 * quad + 4 * PLANES, s, :].bitcast(I32),
                    in_=W1_scales[s * PLANES : (s + 1) * PLANES, 4 * quad : 4 * quad + 4, :].bitcast(I32),
                )

        load_planes(0)
        token_pairs = {0: load_token_pairs(0)}
        load_groups(0, token_pairs[0], slice(GROUPS // 2, GROUPS))
        w_words = keep.tile([P, EXPERTS, H], U32, align_bytes=64)

        def load_weight(e):
            nc.sync.dma_start(
                out=w_words[:, e, :].bitcast(I32),
                in_=W1_words[e].rearrange("p n t -> p (n t)").bitcast(I32),
            )

        for e in range(6):
            load_weight(e)
            if e == 0:
                nc.sync.dma_start(out=rows_gain[0:half_rows, :], in_=g1.rearrange("e (c p) -> (e c) p", p=P))
                nc.sync.dma_start(out=rows_gain[half_rows:P, :], in_=be1.rearrange("e (c p) -> (e c) p", p=P))
            if e == UNITS_PER_ROUND - 1:
                load_planes(1)
                token_rows[1] = load_token_rows(1)

        ident = keep.tile([P, P], BF16)
        make_identity(nc, ident[:])
        ident_f = keep.tile([P, P], F32)
        make_identity(nc, ident_f[:])
        eps_col = keep.tile([P, 1], F32)
        nc.vector.memset(eps_col[:], EPS)
        one_col = keep.tile([P, 1], F32)
        nc.vector.memset(one_col[:], 1.0)
        warm = keep.tile([P, 1], F32)
        nc.scalar.activation(out=warm[:], in_=one_col[:], func=ACT.Exp)
        same_row = keep.tile([P, GROUP_B], F32)
        nc.vector.tensor_reduce(
            out=same_row[:], in_=ident[:].rearrange("p (g b) -> p b g", b=GROUP_B), axis=AX.X, op=ALU.add
        )
        pair_row = keep.tile([P, GROUP_B, AGENTS * SPLIT], BF16)
        nc.vector.tensor_copy(
            out=pair_row[:], in_=same_row[:].unsqueeze(2).to_broadcast([P, GROUP_B, AGENTS * SPLIT])
        )

        def rows_to_columns(rows, name):
            turned = psum.tile([P, P], BF16, tag="bank", name="turned_" + name)
            nc.tensor.transpose(out=turned[:], in_=rows[:], identity=ident[:])
            columns = keep.tile([P, P], BF16, name="columns_" + name)
            nc.scalar.copy(out=columns[:], in_=turned[:])
            return columns

        def spread_vector(columns, first, name):
            bank = psum.tile([P, H], BF16, tag="bank", name=name)
            for c in range(CHUNKS):
                nc.tensor.transpose(
                    out=bank[:, c * P : (c + 1) * P],
                    in_=columns[:, first + c : first + c + 1].to_broadcast([P, P]),
                    identity=ident[:],
                )
            return bank

        columns_bias = rows_to_columns(rows_bias, "bias")
        bias_all = keep.tile([P, EXPERTS, H], BF16)

        def spread_bias(e):
            bias_bank = spread_vector(columns_bias, e * CHUNKS, "bias_bank")
            nc.scalar.copy(out=bias_all[:, e, :], in_=bias_bank[:])

        by_expert = logits_bf[:].rearrange("p t n e -> p t e n")
        wide = [P, B_TILES, EXPERTS, AGENTS]
        top = keep.tile([P, B_TILES, EXPERTS], F32)
        nc.vector.tensor_reduce(out=top[:], in_=by_expert, axis=AX.X, op=ALU.max)
        shifted = keep.tile(wide, F32)
        nc.vector.tensor_tensor(
            out=shifted[:], in0=by_expert, in1=top[:].unsqueeze(3).to_broadcast(wide), op=ALU.subtract
        )
        grown = keep.tile(wide, F32)
        nc.scalar.activation(out=grown[:], in_=shifted[:], func=ACT.Exp)
        total = keep.tile([P, B_TILES, EXPERTS], F32)
        nc.vector.tensor_reduce(out=total[:], in_=grown[:], axis=AX.X, op=ALU.add)
        inverse = keep.tile([P, B_TILES, EXPERTS], F32)
        nc.vector.reciprocal(out=inverse[:], in_=total[:])
        disp = keep.tile(wide, F32)
        nc.vector.tensor_tensor(
            out=disp[:], in0=grown[:], in1=inverse[:].unsqueeze(3).to_broadcast(wide), op=ALU.mult
        )
        hi_lo = keep.tile(wide + [SPLIT], BF16)
        nc.vector.tensor_copy(out=hi_lo[:, :, :, :, 0], in_=disp[:])
        nc.vector.tensor_tensor(out=hi_lo[:, :, :, :, 1], in0=disp[:], in1=hi_lo[:, :, :, :, 0], op=ALU.subtract)

        grouped = {}
        codes = {}
        slot_planes = {}
        for bt in range(B_TILES):
            grouped[bt] = keep.tile([P, EXPERTS, P, PACK], BF16, align_bytes=64, name="grouped%d" % bt)
            codes[bt] = keep.tile([P, EXPERTS, P], U32, align_bytes=64, name="codes%d" % bt)
            slot_planes[bt] = keep.tile([P, EXPERTS, P], U8, align_bytes=64, name="slot_planes%d" % bt)

        def mask_weights(bt, engine):
            shape = [P, PE_EXPERTS, GROUP_B, AGENTS * SPLIT]
            masked = keep.tile(shape, BF16, name="masked%d" % bt)
            engine.tensor_tensor(
                out=masked[:],
                in0=hi_lo[:, bt, 0:PE_EXPERTS].rearrange("p e n s -> p e (n s)").unsqueeze(2).to_broadcast(shape),
                in1=pair_row[:].unsqueeze(1).to_broadcast(shape),
                op=ALU.mult,
            )
            return masked

        def block_diagonal_weights(bt, masked):
            turned = psum.tile([P, PE_EXPERTS, P], BF16, tag="bank", name="turned_weights")
            for e in range(PE_EXPERTS):
                nc.tensor.transpose(
                    out=turned[:, e, :], in_=masked[:, e].rearrange("p b c -> p (b c)"), identity=ident[:]
                )
            diagonal = keep.tile([P, PE_EXPERTS, P], BF16, name="diagonal%d" % bt)
            if bt == 0:
                nc.vector.tensor_copy(out=diagonal[:], in_=turned[:])
            else:
                nc.scalar.copy(out=diagonal[:], in_=turned[:])
            return diagonal

        def tensor_slots(bt, bank_index, diagonal, on_scalar):
            rows = BANK_GROUPS * GROUP_B
            sums = psum.tile([P, PACK, PE_EXPERTS, rows], F32, tag="bank", name="slot_sums")
            for i in range(BANK_GROUPS):
                g = bank_index * BANK_GROUPS + i
                for t in range(PACK):
                    nc.tensor.matmul(
                        out=sums[:, t, :, i * GROUP_B : (i + 1) * GROUP_B],
                        lhsT=token_pairs[bt][:, g, t:D:PACK],
                        rhs=diagonal[:, :, g * GROUP_B : (g + 1) * GROUP_B],
                        start=True,
                        stop=True,
                    )
            target = grouped[bt][:, 0:PE_EXPERTS, bank_index * rows : (bank_index + 1) * rows, :]
            if on_scalar:
                nc.scalar.copy(out=target, in_=sums[:].rearrange("p t e b -> p e b t"))
            else:
                nc.vector.tensor_copy(out=target, in_=sums[:].rearrange("p t e b -> p e b t"))

        row_slots = {}
        for bt in range(B_TILES):
            row_slots[bt] = keep.tile([P, ROW_EXPERTS, D], BF16, name="row_slots%d" % bt)

        running_rows = {}

        def vector_row_slots(bt, i, agents):
            if 0 in agents:
                running_rows[bt] = pool_work.tile([P, D], F32, tag="running", bufs=1, name="running")
            running = running_rows[bt]
            for n in agents:
                weight = disp[:, bt, PE_EXPERTS + i, n : n + 1]
                for cols in (slice(0, D // 2), slice(D // 2, D)):
                    if n == 0:
                        nc.vector.tensor_scalar(
                            out=running[:, cols], in0=token_rows[bt][:, n, cols], scalar1=weight, scalar2=None,
                            op0=ALU.mult,
                        )
                    else:
                        target = running[:, cols] if n < AGENTS - 1 else row_slots[bt][:, i, cols]
                        nc.vector.scalar_tensor_tensor(
                            out=target, in0=token_rows[bt][:, n, cols], scalar=weight, in1=running[:, cols],
                            op0=ALU.mult, op1=ALU.add,
                        )

        pool_running = {}

        def pool_row_slots(bt, i, agents):
            if 0 in agents:
                pool_running[(bt, i)] = pool_work.tile([P, 2, D], F32, tag="pool_running", bufs=1, name="pool_running")
            running = pool_running[(bt, i)]
            for first in agents[::2]:
                pair = running if first == 0 else pool_work.tile([P, 2, D], F32, tag="product", name="product")
                for a in range(2):
                    weight = disp[:, bt, PE_EXPERTS + i, first + a : first + a + 1]
                    nc.gpsimd.tensor_scalar(
                        out=pair[:, a, :], in0=token_rows[bt][:, first + a, :], scalar1=weight, scalar2=0.0,
                        op0=ALU.mult, op1=ALU.add,
                    )
                if first > 0:
                    nc.gpsimd.tensor_tensor(out=running[:], in0=running[:], in1=pair[:], op=ALU.add)
            if AGENTS - 1 in agents:
                nc.gpsimd.tensor_tensor(
                    out=row_slots[bt][:, i, :], in0=running[:, 0, :], in1=running[:, 1, :], op=ALU.add
                )

        def turn_row_slots(bt):
            turned = psum.tile([P, ROW_EXPERTS, P, PACK // 2], F32, tag="bank", name="turned_slots")
            for i in range(ROW_EXPERTS):
                words = row_slots[bt][:, i, :].bitcast(F32)
                for s in range(PACK // 2):
                    nc.tensor.transpose(
                        out=turned[:, i, :, s], in_=words[:, s : D // 2 : PACK // 2], identity=ident_f[:]
                    )
            nc.vector.tensor_copy(
                out=grouped[bt][:, PE_EXPERTS:EXPERTS, :, :].rearrange("p e b t -> p (e b t)").bitcast(F32),
                in_=turned[:].rearrange("p e b s -> p (e b s)"),
            )

        def quantise_pair(bt, e):
            pair = slice(e, e + 2)
            nc.vector.quantize_mx(
                out=codes[bt][:, pair, :].rearrange("p e b -> p (e b)").bitcast(FP8X4),
                scales=slot_planes[bt][:, pair, :].rearrange("p e b -> p (e b)"),
                in_=grouped[bt][:, pair, :, :].rearrange("p e b t -> p (e b t)"),
            )

        units = [(bt, e) for bt in range(B_TILES) for e in range(EXPERTS)]
        rounds = [units[i : i + UNITS_PER_ROUND] for i in range(0, len(units), UNITS_PER_ROUND)]
        last_round = len(rounds) - 1
        def round_units(r):
            return rounds[r] if 0 <= r < len(rounds) else []

        hidden = {}
        centred = {}
        curve = {}
        squares = {}
        moments = {}
        log_var = {}
        rstd = {}

        def vector_takes_variance(unit):
            place = units.index(unit)
            return place >= UNITS_PER_ROUND and place % 2 == 1 or place in (10, 14)

        late = []

        def run_late():
            while late:
                late.pop(0)()

        layer_sums = {}
        halves = [slice(half * BANK, (half + 1) * BANK) for half in range(H // BANK)]

        def multiply(unit):
            bt, e = unit
            layer_sums[unit] = []
            for cols in halves:
                sums = psum.tile([P, BANK], F32, tag="bank", name="layer_sums")
                nc.tensor.matmul_mx(
                    out=sums[:],
                    lhsT=codes[bt][:, e, :].bitcast(FP8X4),
                    lhsT_scale=slot_planes[bt][:, e, :],
                    rhs=w_words[:, e, cols].bitcast(FP8X4),
                    rhs_scale=w_planes[4 * (e % PLANES) : P, e // PLANES, cols],
                    start=True,
                    stop=True,
                )
                layer_sums[unit].append(sums)

        def add_bias_and_sum(r, j, unit):
            bt, e = unit
            hidden[unit] = work.tile([P, H], F32, tag="hidden", bufs=UNITS_PER_ROUND, name="hidden")
            h = hidden[unit]
            if not vector_takes_variance(unit):
                h_sums = small.tile([P, 2], F32, tag="h_sums", name="h_sums")
            for half, cols in enumerate(halves):
                sums = layer_sums[unit][half]
                if vector_takes_variance(unit):
                    nc.vector.tensor_tensor(out=h[:, cols], in0=sums[:], in1=bias_all[:, e, cols], op=ALU.add)
                else:
                    nc.vector.scalar_tensor_tensor(
                        out=h[:, cols], in0=sums[:], scalar=1.0, in1=bias_all[:, e, cols],
                        op0=ALU.mult, op1=ALU.add, accum_out=h_sums[:, half : half + 1],
                    )
                run_late()
            if vector_takes_variance(unit):
                h_stats = small.tile([P, 2, 6], F32, tag="h_stats", name="h_stats")
                for half, cols in enumerate(halves):
                    nc.vector.bn_stats(out=h_stats[:, half, :], in_=h[:, cols])
                late.append(lambda: nc.vector.bn_aggr(
                    out=moments[r][:, j, :], in_=h_stats[:].rearrange("p a b -> p (a b)")
                ))
            else:
                late.append(lambda: mean_and_squares(r, j, unit, h_sums))

        def mean_and_squares(r, j, unit, h_sums):
            nc.vector.tensor_scalar(
                out=moments[r][:, j, 0:1], in0=h_sums[:, 0:1], scalar1=h_sums[:, 1:2], scalar2=1.0 / H,
                op0=ALU.add, op1=ALU.mult,
            )
            unread = work.tile([P, H], BF16, tag="unread", bufs=2, name="unread")
            nc.scalar.activation(
                out=unread[:], in_=hidden[unit][:], func=ACT.Square, bias=moments[r][:, j, 0:1], scale=-1.0,
                accum_out=squares[r][:, j : j + 1],
            )

        def centre_and_gain(r, j, unit):
            bt, e = unit
            gain_bank = spread_vector(columns_gain, e * CHUNKS, "gain_bank")
            centred[unit] = work.tile([P, H], F32, tag="centred", bufs=CENTRED_BUFS, name="centred")
            nc.vector.scalar_tensor_tensor(
                out=centred[unit][:], in0=hidden[unit][:], scalar=moments[r][:, j, 0:1], in1=gain_bank[:],
                op0=ALU.subtract, op1=ALU.mult,
            )

        def log_variance(r):
            log_var[r] = small.tile([P, UNITS_PER_ROUND], F32, tag="log_var", name="log_var")
            by_vector = [j for j, unit in enumerate(rounds[r]) if vector_takes_variance(unit)]
            by_scalar = [j for j in range(UNITS_PER_ROUND) if j not in by_vector]
            for columns, source, scale in ((by_scalar, squares[r], 1.0 / H), (by_vector, moments[r][:, :, 1], 1.0)):
                if columns:
                    step = columns[1] - columns[0] if len(columns) > 1 else 1
                    some = slice(columns[0], columns[-1] + 1, step)
                    nc.scalar.activation(
                        out=log_var[r][:, some], in_=source[:, some], func=ACT.Ln, bias=eps_col[:], scale=scale
                    )

        def scale_shift_and_exp(r, j, unit):
            bt, e = unit
            shift_bank = spread_vector(columns_gain, (EXPERTS + e) * CHUNKS, "shift_bank")
            v = centred[unit]
            last = r == last_round
            nc.vector.scalar_tensor_tensor(
                out=v[:], in0=v[:], scalar=rstd[r][:, j : j + 1], in1=shift_bank[:],
                op0=ALU.mult, op1=ALU.subtract if last else ALU.add,
            )
            curve[unit] = work.tile([P, H], F32, tag="curve", name="curve")
            nc.scalar.activation(out=curve[unit][:], in_=v[:], func=ACT.Exp, scale=-1.0 if last else 1.0)

        def first_product(unit):
            u = curve[unit]
            nc.vector.scalar_tensor_tensor(
                out=u[:], in0=u[:], scalar=2.0, in1=u[:], op0=ALU.add, op1=ALU.mult
            )

        def root(unit):
            nc.scalar.activation(
                out=curve[unit][:], in_=curve[unit][:], func=ACT.Abs_reciprocal_sqrt, bias=one_col[:], scale=0.5
            )

        def square_of_root(j, unit):
            c = curve[unit]
            if j >= UNITS_PER_ROUND // 2:
                nc.scalar.activation(out=c[:], in_=c[:], func=ACT.Square)
            else:
                nc.vector.tensor_tensor(out=c[:], in0=c[:], in1=c[:], op=ALU.mult)

        def last_product(unit):
            bt, e = unit
            for cols in (slice(0, H // 2), slice(H // 2, H)):
                nc.vector.scalar_tensor_tensor(
                    out=curve[unit][:, cols], in0=curve[unit][:, cols], scalar=1.0, in1=centred[unit][:, cols],
                    op0=ALU.subtract, op1=ALU.mult,
                )
                nc.sync.dma_start(out=out[bt * P : (bt + 1) * P, e, cols], in_=curve[unit][:, cols])

        def finish(r, unit):
            nc.scalar.activation(out=curve[unit][:], in_=curve[unit][:], func=ACT.Tanh)
            if not vector_takes_product(unit):
                product(nc.gpsimd, unit)

        def vector_takes_product(unit):
            return unit in rounds[last_round - 1][UNITS_PER_ROUND // 2 :]

        def product(engine, unit):
            bt, e = unit
            engine.tensor_tensor(out=curve[unit][:], in0=curve[unit][:], in1=centred[unit][:], op=ALU.mult)
            nc.sync.dma_start(out=out[bt * P : (bt + 1) * P, e, :], in_=curve[unit][:])

        for e in range(UNITS_PER_ROUND):
            spread_bias(e)
        masked = [mask_weights(0, nc.vector), mask_weights(1, nc.gpsimd)]
        vector_row_slots(0, 0, range(2))
        diagonal = [block_diagonal_weights(0, masked[0])]
        vector_row_slots(0, 0, range(2, AGENTS))
        pool_row_slots(0, 1, range(AGENTS))
        for bank_index in range(ROUTE_BANKS):
            tensor_slots(0, bank_index, diagonal[0], bank_index not in (5, 7))
        for e in range(UNITS_PER_ROUND, 6):
            spread_bias(e)
        columns_gain = rows_to_columns(rows_gain, "gain")
        nc.scalar.activation(out=warm[:], in_=one_col[:], func=ACT.Ln)
        for e in range(0, PE_EXPERTS, 2):
            quantise_pair(0, e)
        token_pairs[1] = load_token_pairs(1)
        load_groups(1, token_pairs[1], slice(GROUPS // 2, GROUPS))
        for e in range(6, EXPERTS):
            load_weight(e)
        pool_row_slots(1, 0, range(AGENTS))
        pool_row_slots(1, 1, range(AGENTS // 2))

        for r in range(-2, len(rounds)):
            if round_units(r + 1):
                rstd[r + 1] = small.tile([P, UNITS_PER_ROUND], F32, tag="rstd", name="rstd")
                nc.scalar.activation(out=rstd[r + 1][:], in_=log_var[r + 1][:], func=ACT.Exp, scale=-0.5)
            if r + 1 == 0:
                diagonal.append(block_diagonal_weights(1, masked[1]))
                for e in range(6, EXPERTS):
                    spread_bias(e)
            for j, unit in enumerate(round_units(r)):
                if r == last_round:
                    square_of_root(j, unit)
                else:
                    finish(r, unit)
            if r == last_round:
                for unit in round_units(r):
                    last_product(unit)
            if r == 0:
                pool_row_slots(1, 1, range(AGENTS // 2, AGENTS))
            if r + 1 == last_round:
                nc.vector.tensor_scalar(
                    out=rstd[r + 1][:], in0=rstd[r + 1][:], scalar1=-1.0, scalar2=None, op0=ALU.mult
                )
            for j, unit in enumerate(round_units(r + 1)):
                scale_shift_and_exp(r + 1, j, unit)
            if r + 1 == last_round:
                for unit in round_units(r + 1):
                    first_product(unit)
                for unit in round_units(r):
                    if vector_takes_product(unit):
                        product(nc.vector, unit)

            if round_units(r + 2):
                squares[r + 2] = small.tile([P, UNITS_PER_ROUND], F32, tag="squares", name="squares")
                moments[r + 2] = small.tile([P, UNITS_PER_ROUND, 2], F32, tag="moments", name="moments")
            for j in range(UNITS_PER_ROUND):
                if round_units(r + 2):
                    bt, e = round_units(r + 2)[j]
                    multiply((bt, e))
                    if e == PE_EXPERTS - 1:
                        turn_row_slots(bt)
                        quantise_pair(bt, PE_EXPERTS)
                    add_bias_and_sum(r + 2, j, (bt, e))
                    if r + 2 == 1:
                        tensor_slots(1, 2 * j, diagonal[1], False)
                        tensor_slots(1, 2 * j + 1, diagonal[1], True)
                if round_units(r + 1):
                    unit = round_units(r + 1)[j]
                    if r + 1 == last_round:
                        root(unit)
                    else:
                        nc.scalar.activation(
                            out=curve[unit][:], in_=curve[unit][:], func=ACT.Ln, bias=one_col[:], scale=1.0
                        )
            for j, unit in enumerate(round_units(r + 2)):
                centre_and_gain(r + 2, j, unit)
                if j == 0:
                    run_late()
                    log_variance(r + 2)
            if r + 2 == 1:
                for e in range(0, PE_EXPERTS, 2):
                    quantise_pair(1, e)
